import numpy as np
import ml_dtypes


def mxq(x, axis, fmt="e4m3"):
    dtype, down = {"e4m3": (ml_dtypes.float8_e4m3fn, 7), "e5m2": (ml_dtypes.float8_e5m2, 14)}[fmt]
    v = np.moveaxis(np.asarray(x, np.float32).astype(ml_dtypes.bfloat16).astype(np.float64), axis, -1)
    blocks = v.reshape(v.shape[:-1] + (-1, 32))
    amax = np.abs(blocks).max(-1, keepdims=True)
    byte = np.maximum(np.where(amax > 0, np.frexp(amax)[1] - 1 + 127, 0) - down, 1)
    scale = np.exp2(byte - 127.0)
    codes = (blocks / scale).astype(np.float32).astype(dtype).astype(np.float64)
    return np.moveaxis((codes * scale).reshape(v.shape), -1, axis)


WIDE = False


def mx_kscale(k):
    if not WIDE:
        return np.ones(k)
    levels = np.array([10, -10, 5, -5, 0])
    a = np.random.permutation(np.resize(levels, k // 512 * 4)).reshape(k // 512, 4)
    idx = np.arange(k)
    return np.exp2(a[idx // 512, idx % 128 // 32])


BF16 = ml_dtypes.bfloat16


def bf(x):
    return np.asarray(x, np.float32).astype(BF16)


def f64(x):
    return np.asarray(x).astype(np.float64)


E2M1 = np.array([0.0, 0.5, 1.0, 1.5, 2.0, 3.0, 4.0, 6.0, -0.0, -0.5, -1.0, -1.5, -2.0, -3.0, -4.0, -6.0])


def pack_weight(w, fmt):
    k, n = w.shape
    w = f64(bf(w)).reshape(k // 32, 32, n)
    amax = np.abs(w).max(1)
    if fmt == "e4m3":
        byte = np.frexp(amax)[1] - 1 + 127 - 7
    else:
        mant, ex = np.frexp(amax / 6.0)
        byte = np.where(mant > 0.5, ex, ex - 1) + 127
    byte = np.clip(np.where(amax > 0, byte, 1), 1, 254)
    scaled = (w * np.exp2(127.0 - byte)[:, None, :]).reshape(k, n).astype(np.float32)
    by_word = np.ascontiguousarray(scaled.reshape(k // 512, 128, 4, n).transpose(0, 1, 3, 2))
    if fmt == "e4m3":
        words = by_word.astype(ml_dtypes.float8_e4m3fn).view(np.uint8)
    else:
        c = by_word.astype(ml_dtypes.float4_e2m1fn).view(np.uint8) & 0xF
        words = c[..., 0::2] | (c[..., 1::2] << 4)
    return np.ascontiguousarray(words), np.ascontiguousarray(byte.astype(np.uint8).reshape(k // 512, 16, n))


def unpack_weight(words, scales, fmt):
    g, p, n, _ = words.shape
    if fmt == "e4m3":
        vals = np.ascontiguousarray(words).view(ml_dtypes.float8_e4m3fn).astype(np.float64)
    else:
        nib = np.empty((g, p, n, 4), np.uint8)
        nib[..., 0::2] = words & 0xF
        nib[..., 1::2] = words >> 4
        vals = E2M1[nib]
    vals = vals * np.repeat(np.exp2(scales.astype(np.float64) - 127.0), 8, axis=1)[..., None]
    return vals.transpose(0, 1, 3, 2).reshape(g * 512, n)

def pack4(w):
    words, scales = pack_weight(w, "e2m1")
    return words.reshape(words.shape[0], 128, -1), scales


def unpack4(words, scales):
    return unpack_weight(words.reshape(words.shape[0], 128, -1, 2), scales, "e2m1")


B, L, C, K = 512, 8, 512, 5
F = C
BN_EPS = 1e-3
LEAKY_ALPHA = 0.3


def leaky(v):
    return np.where(v >= 0, v, LEAKY_ALPHA * v)


def bn(v, gamma, beta, mean, var):
    return gamma * (v - mean) * (1.0 / np.sqrt(var + BN_EPS)) + beta


def setup_inputs():
    s = mx_kscale(F)
    h = bf(leaky(np.random.standard_normal((B, L, F)) * 1.2) * s)
    x = bf(np.random.standard_normal((B, L, C)))
    k2 = np.random.standard_normal((K, L, F, F)) * 0.16 / np.sqrt(K * F) / s[:, None]
    k2_words, k2_scales = pack4(k2.reshape(-1, F))
    return {"h": h,
            "x": x,
            "k2_words": k2_words,
            "k2_scales": k2_scales,
            "b2": bf(np.random.standard_normal((L, F)) * 0.03),
            "gamma2": bf(1.0 + 0.1 * np.random.standard_normal(F)),
            "beta2": bf(np.random.standard_normal(F) * 0.2),
            "mean2": bf(np.random.standard_normal(F) * 0.05),
            "var2": bf(np.random.uniform(0.01, 0.03, F))}


def reference(h, x, k2_words, k2_scales, b2, gamma2, beta2, mean2, var2):
    hq = mxq(f64(h).transpose(1, 0, 2), 2, "e4m3")
    k = unpack4(k2_words, k2_scales).reshape(K, L, F, F)
    out = 2.0 * f64(b2)
    for i in range(k.shape[0]):
        step = (i // 2) * (-1 if i % 2 == 1 else 1)
        ki = k[i][(np.arange(L) + step) % L] if step != 0 else k[i]
        p = hq @ ki
        p = np.roll(p, step, axis=0) if step != 0 else p
        out = out + p.transpose(1, 0, 2)
    return leaky(bn(out, f64(gamma2), f64(beta2), f64(mean2), f64(var2)) + f64(x))

@@ -1,0 +1,201 @@
+from contextlib import ExitStack
+
+import concourse.mybir as mybir
+from concourse.masks import make_identity
+
+F32 = mybir.dt.float32
+BF16 = mybir.dt.bfloat16
+I32 = mybir.dt.int32
+U32 = mybir.dt.uint32
+U8 = mybir.dt.uint8
+FP8X4 = mybir.dt.float8_e4m3fn_x4
+FP4X4 = mybir.dt.float4_e2m1fn_x4
+ALU = mybir.AluOpType
+ACT = mybir.ActivationFunctionType
+
+P = 128
+B = 512
+L = 8
+C = 512
+TAPS = 5
+STEP = (0, 0, 1, -1, 2)
+BN_EPS = 1e-3
+LEAKY_ALPHA = 0.3
+B_TILES = B // P
+F_TILES = C // P
+PAIRS = L // 2
+
+FLOPS = 2 * B * L * TAPS * C * C
+
+ROW_GAMMA, ROW_BETA, ROW_MEAN, ROW_VAR, PARAM_ROWS = L, L + 1, L + 2, L + 3, L + 4
+
+
+def tile_residualblock5_pb_t_e_kernel(
+    tc, h, x, k2_words, k2_scales, b2, gamma2, beta2, mean2, var2, out
+):
+    nc = tc.nc
+
+    h_pairs = h.rearrange("(t p) l c -> p t (l c)", p=P)
+    x_pairs = x.rearrange("(t p) l f -> p t (l f)", p=P)
+    out_by_l = out.rearrange("(t p) l f -> l p t f", p=P)
+    words_by_l = k2_words.bitcast(I32).rearrange("(i l) p w -> l p i w", l=L)
+    scales_by_l = k2_scales.bitcast(I32).rearrange("(i l) (q r) n -> l r q i n", l=L, r=4)
+
+    with ExitStack() as ctx:
+        ctx.enter_context(tc.manual_schedule())
+        keep = ctx.enter_context(tc.tile_pool(name="keep", bufs=1))
+        stage = ctx.enter_context(tc.tile_pool(name="stage", bufs=2))
+        norm_pool = ctx.enter_context(tc.tile_pool(name="norm", bufs=2))
+        out_pool = ctx.enter_context(tc.tile_pool(name="outs", bufs=4))
+        acc_pool = ctx.enter_context(tc.psum_pool(name="acc", bufs=3))
+        turn_pool = ctx.enter_context(tc.psum_pool(name="turn", bufs=5))
+
+        ident_f32 = keep.tile([P, P], F32, name="ident_f32")
+        ident_bf16 = keep.tile([P, P], BF16, name="ident_bf16")
+        params = keep.tile([P, C], BF16, name="params")
+        h_raw = [keep.tile([P, B_TILES, 2 * C], BF16, name="h_raw%d" % q) for q in range(PAIRS)]
+        x_sb = [keep.tile([P, B_TILES, 2 * C], BF16, name="x_sb%d" % q) for q in range(PAIRS)]
+        w_words = [keep.tile([P, TAPS, 2 * C], U8, name="w_words%d" % l, align_bytes=64) for l in range(L)]
+        w_scales = [keep.tile([P, TAPS, C], U8, name="w_scales%d" % l, align_bytes=64) for l in range(L)]
+        h_codes = [keep.tile([P, B], U32, name="h_codes%d" % m, align_bytes=64) for m in range(L)]
+        h_scales = [keep.tile([P, B], U8, name="h_scales%d" % m, align_bytes=64) for m in range(L)]
+
+        make_identity(nc, ident_f32[:])
+        make_identity(nc, ident_bf16[:])
+
+        nc.vector.memset(params[:], 0.0)
+        for l in range(L):
+            nc.vector.memset(w_scales[l][:].bitcast(I32), 0)
+
+        def load_h(q):
+            nc.sync.dma_start(out=h_raw[q][:], in_=h_pairs[:, :, 2 * C * q : 2 * C * (q + 1)])
+
+        def load_x(q):
+            nc.sync.dma_start(out=x_sb[q][:], in_=x_pairs[:, :, 2 * C * q : 2 * C * (q + 1)])
+
+        def load_weights(l):
+            for r in range(4):
+                nc.sync.dma_start(out=w_scales[l][r:P:32].bitcast(I32), in_=scales_by_l[l, r])
+            nc.sync.dma_start(out=w_words[l][:].bitcast(I32), in_=words_by_l[l])
+
+        nc.scalar.dma_start(out=params[0:L, :], in_=b2)
+        nc.scalar.dma_start(out=params[ROW_GAMMA : ROW_GAMMA + 1, :], in_=gamma2.unsqueeze(0))
+        nc.scalar.dma_start(out=params[ROW_BETA : ROW_BETA + 1, :], in_=beta2.unsqueeze(0))
+        nc.scalar.dma_start(out=params[ROW_MEAN : ROW_MEAN + 1, :], in_=mean2.unsqueeze(0))
+        nc.scalar.dma_start(out=params[ROW_VAR : ROW_VAR + 1, :], in_=var2.unsqueeze(0))
+
+        load_h(0)
+        load_h(3)
+        load_weights(0)
+        load_h(1)
+        load_weights(1)
+        load_x(0)
+        load_weights(2)
+        load_h(2)
+        load_weights(3)
+        load_x(1)
+        load_weights(4)
+        load_weights(5)
+        load_x(2)
+        load_weights(6)
+        load_weights(7)
+        load_x(3)
+
+        params_ps = turn_pool.tile([P, F_TILES, P], BF16, tag="turn")
+        for j in range(F_TILES):
+            nc.tensor.transpose(params_ps[:, j, :], params[:, P * j : P * (j + 1)], ident_bf16[:])
+        by_filter = keep.tile([P, F_TILES, PARAM_ROWS], F32, name="by_filter")
+        nc.vector.tensor_copy(out=by_filter[:], in_=params_ps[:, :, 0:PARAM_ROWS])
+        std = keep.tile([P, F_TILES], F32, name="std")
+        bn_scale = keep.tile([P, F_TILES], F32, name="bn_scale")
+        bn_shift = keep.tile([P, F_TILES, L], F32, name="bn_shift")
+        wide = [P, F_TILES, L]
+        nc.vector.tensor_scalar_add(out=std[:], in0=by_filter[:, :, ROW_VAR], scalar1=BN_EPS)
+        nc.scalar.sqrt(out=std[:], in_=std[:])
+        nc.vector.reciprocal(out=bn_scale[:], in_=std[:])
+        nc.vector.tensor_mul(out=bn_scale[:], in0=bn_scale[:], in1=by_filter[:, :, ROW_GAMMA])
+        nc.vector.scalar_tensor_tensor(
+            out=bn_shift[:],
+            in0=by_filter[:, :, 0:L],
+            scalar=2.0,
+            in1=by_filter[:, :, ROW_MEAN : ROW_MEAN + 1].to_broadcast(wide),
+            op0=ALU.mult,
+            op1=ALU.subtract,
+        )
+        nc.vector.tensor_mul(out=bn_shift[:], in0=bn_shift[:], in1=bn_scale[:].unsqueeze(2).to_broadcast(wide))
+        nc.vector.tensor_add(
+            out=bn_shift[:], in0=bn_shift[:], in1=by_filter[:, :, ROW_BETA : ROW_BETA + 1].to_broadcast(wide)
+        )
+
+        def quantise_position(m):
+            words = h_raw[m // 2][:].bitcast(F32)
+            first = (C // 2) * (m % 2)
+            grouped = stage.tile([P, 4 * B], BF16, align_bytes=64)
+            grouped_words = grouped[:].bitcast(F32).rearrange("p (t b u) -> p t b u", t=B_TILES, u=2)
+            for half in range(2):
+                bank = turn_pool.tile([P, 2, 2, P], F32, tag="turn")
+                for s in range(2):
+                    for u in range(2):
+                        nc.tensor.transpose(
+                            bank[:, s, u, :], words[:, 2 * half + s, first + u : first + C // 2 : 2], ident_f32[:]
+                        )
+                copy = nc.scalar.copy if half == 0 else nc.vector.tensor_copy
+                copy(out=grouped_words[:, 2 * half : 2 * half + 2], in_=bank[:].rearrange("p s u b -> p s b u"))
+            nc.vector.quantize_mx(out=h_codes[m][:].bitcast(FP8X4), scales=h_scales[m][:], in_=grouped[:])
+
+        def multiply(l, j, normed):
+            acc = acc_pool.tile([P, B], F32, tag="acc")
+            for i in range(TAPS):
+                m = (l - STEP[i]) % L
+                nc.tensor.matmul_mx(
+                    out=acc[:],
+                    lhsT=w_words[l][:, i, 2 * P * j : 2 * P * (j + 1)].bitcast(FP4X4),
+                    lhsT_scale=w_scales[l][:, i, P * j : P * (j + 1)],
+                    rhs=h_codes[m][:].bitcast(FP8X4),
+                    rhs_scale=h_scales[m][:],
+                    start=(i == 0),
+                    stop=(i == TAPS - 1),
+                )
+            nc.scalar.activation(
+                out=normed[:, j, :],
+                in_=acc[:],
+                func=ACT.Identity,
+                bias=bn_shift[:, j, l : l + 1],
+                scale=bn_scale[:, j : j + 1],
+            )
+
+        def finish(l, normed):
+            result = out_pool.tile([P, B_TILES, C], F32)
+            x_l = x_sb[l // 2][:, :, C * (l % 2) : C * (l % 2 + 1)]
+            for half in range(2):
+                pair = slice(2 * half, 2 * half + 2)
+                for t in range(2 * half, 2 * half + 2):
+                    bank = turn_pool.tile([P, C], F32, tag="turn")
+                    for j in range(F_TILES):
+                        nc.tensor.transpose(
+                            bank[:, P * j : P * (j + 1)], normed[:, j, P * t : P * (t + 1)], ident_f32[:]
+                        )
+                    nc.vector.tensor_tensor(out=result[:, t, :], in0=bank[:], in1=x_l[:, t, :], op=ALU.add)
+                nc.vector.scalar_tensor_tensor(
+                    out=result[:, pair, :],
+                    in0=result[:, pair, :],
+                    scalar=LEAKY_ALPHA,
+                    in1=result[:, pair, :],
+                    op0=ALU.mult,
+                    op1=ALU.max,
+                )
+                nc.sync.dma_start(out=out_by_l[l][:, pair, :], in_=result[:, pair, :])
+
+        for m in (0, 1, 6, 7):
+            quantise_position(m)
+        normed_of = {}
+        for l in range(L):
+            normed_of[l] = norm_pool.tile([P, F_TILES, B], F32, name="normed")
+            for j in range(F_TILES):
+                multiply(l, j, normed_of[l])
+                if j == 0:
+                    if 2 <= l + 2 <= 5:
+                        quantise_position(l + 2)
+                    if l >= 1:
+                        finish(l - 1, normed_of[l - 1])
+        finish(L - 1, normed_of[L - 1])

@@ -21,9 +21,17 @@ TAPS = 5
 STEP = (0, 0, 1, -1, 2)
 BN_EPS = 1e-3
 LEAKY_ALPHA = 0.3
-B_TILES = B // P
-F_TILES = C // P
-PAIRS = L // 2
+TILES = 4
+
+BATCH_MAJOR = (0, 2, 4, 6, 7)
+FILTER_MAJOR = (1, 3, 5)
+LAG = TILES * (len(BATCH_MAJOR) - len(FILTER_MAJOR))
+BATCH_GROUPS = [(l, t) for l in BATCH_MAJOR for t in range(TILES)]
+FILTER_GROUPS = [(l, j) for l in FILTER_MAJOR for j in range(TILES)]
+
+UNITS = [(q, t) for t in range(TILES) for q in (0, 3)] + [(q, t) for q in (1, 2) for t in range(TILES)]
+UNITS_AHEAD = 4
+UNITS_PER_STEP = 2
 
 FLOPS = 2 * B * L * TAPS * C * C
 
@@ -35,8 +43,8 @@ def tile_residualblock5_pb_t_e_kernel(
 ):
     nc = tc.nc
 
-    h_pairs = h.rearrange("(t p) l c -> p t (l c)", p=P)
-    x_pairs = x.rearrange("(t p) l f -> p t (l f)", p=P)
+    h_pairs = h.rearrange("(t p) (q e) c -> p t q (e c)", p=P, e=2)
+    x_by_l = x.rearrange("(t p) l f -> l p t f", p=P)
     out_by_l = out.rearrange("(t p) l f -> l p t f", p=P)
     words_by_l = k2_words.bitcast(I32).rearrange("(i l) p w -> l p i w", l=L)
     scales_by_l = k2_scales.bitcast(I32).rearrange("(i l) (q r) n -> l r q i n", l=L, r=4)
@@ -44,17 +52,19 @@ def tile_residualblock5_pb_t_e_kernel(
     with ExitStack() as ctx:
         ctx.enter_context(tc.manual_schedule())
         keep = ctx.enter_context(tc.tile_pool(name="keep", bufs=1))
-        stage = ctx.enter_context(tc.tile_pool(name="stage", bufs=2))
-        norm_pool = ctx.enter_context(tc.tile_pool(name="norm", bufs=2))
-        out_pool = ctx.enter_context(tc.tile_pool(name="outs", bufs=4))
-        acc_pool = ctx.enter_context(tc.psum_pool(name="acc", bufs=3))
-        turn_pool = ctx.enter_context(tc.psum_pool(name="turn", bufs=5))
+        stage = ctx.enter_context(tc.tile_pool(name="stage", bufs=3))
+        ahead = ctx.enter_context(tc.tile_pool(name="ahead", bufs=2))
+        out_pool = ctx.enter_context(tc.tile_pool(name="outs", bufs=5))
+        acc_pool = ctx.enter_context(tc.psum_pool(name="acc", bufs=4))
+        turn_pool = ctx.enter_context(tc.psum_pool(name="turn", bufs=4))
 
         ident_f32 = keep.tile([P, P], F32, name="ident_f32")
         ident_bf16 = keep.tile([P, P], BF16, name="ident_bf16")
         params = keep.tile([P, C], BF16, name="params")
-        h_raw = [keep.tile([P, B_TILES, 2 * C], BF16, name="h_raw%d" % q) for q in range(PAIRS)]
-        x_sb = [keep.tile([P, B_TILES, 2 * C], BF16, name="x_sb%d" % q) for q in range(PAIRS)]
+        h_ends = keep.tile([P, TILES, 2, 2 * C], BF16, name="h_ends")
+        h_mid = keep.tile([P, 2, TILES, 2 * C], BF16, name="h_mid")
+        h_raw = {0: h_ends[:, :, 0, :], 1: h_mid[:, 0], 2: h_mid[:, 1], 3: h_ends[:, :, 1, :]}
+        x_sb = [keep.tile([P, TILES, C], BF16, name="x_sb%d" % l) for l in range(L)]
         w_words = [keep.tile([P, TAPS, 2 * C], U8, name="w_words%d" % l, align_bytes=64) for l in range(L)]
         w_scales = [keep.tile([P, TAPS, C], U8, name="w_scales%d" % l, align_bytes=64) for l in range(L)]
         h_codes = [keep.tile([P, B], U32, name="h_codes%d" % m, align_bytes=64) for m in range(L)]
@@ -64,86 +74,147 @@ def tile_residualblock5_pb_t_e_kernel(
         make_identity(nc, ident_bf16[:])
 
         nc.vector.memset(params[:], 0.0)
+        one = keep.tile([P, 1], F32, name="one")
+        nc.vector.memset(one[:], 1.0)
         for l in range(L):
             nc.vector.memset(w_scales[l][:].bitcast(I32), 0)
 
-        def load_h(q):
-            nc.sync.dma_start(out=h_raw[q][:], in_=h_pairs[:, :, 2 * C * q : 2 * C * (q + 1)])
+        def load_h_ends(t):
+            nc.sync.dma_start(out=h_ends[:, t], in_=h_pairs[:, t, 0:4:3, :])
 
-        def load_x(q):
-            nc.sync.dma_start(out=x_sb[q][:], in_=x_pairs[:, :, 2 * C * q : 2 * C * (q + 1)])
+        def load_h_mid(q):
+            nc.sync.dma_start(out=h_mid[:, q - 1], in_=h_pairs[:, :, q, :])
+
+        def load_x(l):
+            nc.sync.dma_start(out=x_sb[l][:], in_=x_by_l[l])
 
         def load_weights(l):
             for r in range(4):
                 nc.sync.dma_start(out=w_scales[l][r:P:32].bitcast(I32), in_=scales_by_l[l, r])
             nc.sync.dma_start(out=w_words[l][:].bitcast(I32), in_=words_by_l[l])
 
-        nc.scalar.dma_start(out=params[0:L, :], in_=b2)
-        nc.scalar.dma_start(out=params[ROW_GAMMA : ROW_GAMMA + 1, :], in_=gamma2.unsqueeze(0))
-        nc.scalar.dma_start(out=params[ROW_BETA : ROW_BETA + 1, :], in_=beta2.unsqueeze(0))
-        nc.scalar.dma_start(out=params[ROW_MEAN : ROW_MEAN + 1, :], in_=mean2.unsqueeze(0))
-        nc.scalar.dma_start(out=params[ROW_VAR : ROW_VAR + 1, :], in_=var2.unsqueeze(0))
+        def load_params():
+            nc.scalar.dma_start(out=params[0:L, :], in_=b2)
+            nc.scalar.dma_start(out=params[ROW_GAMMA : ROW_GAMMA + 1, :], in_=gamma2.unsqueeze(0))
+            nc.scalar.dma_start(out=params[ROW_BETA : ROW_BETA + 1, :], in_=beta2.unsqueeze(0))
+            nc.scalar.dma_start(out=params[ROW_MEAN : ROW_MEAN + 1, :], in_=mean2.unsqueeze(0))
+            nc.scalar.dma_start(out=params[ROW_VAR : ROW_VAR + 1, :], in_=var2.unsqueeze(0))
 
-        load_h(0)
-        load_h(3)
+        load_h_ends(0)
+        load_h_ends(1)
         load_weights(0)
-        load_h(1)
-        load_weights(1)
+        load_params()
+        nc.scalar.sqrt(out=one[:], in_=one[:])
+        load_h_ends(2)
         load_x(0)
-        load_weights(2)
-        load_h(2)
-        load_weights(3)
-        load_x(1)
-        load_weights(4)
-        load_weights(5)
+        load_h_ends(3)
+        load_h_mid(1)
         load_x(2)
-        load_weights(6)
-        load_weights(7)
-        load_x(3)
+        load_weights(2)
+        load_h_mid(2)
+        for l_batch, l_filter in zip(BATCH_MAJOR[2:], FILTER_MAJOR):
+            load_x(l_batch)
+            load_weights(l_batch)
+            load_weights(l_filter)
+            load_x(l_filter)
 
-        params_ps = turn_pool.tile([P, F_TILES, P], BF16, tag="turn")
-        for j in range(F_TILES):
-            nc.tensor.transpose(params_ps[:, j, :], params[:, P * j : P * (j + 1)], ident_bf16[:])
-        by_filter = keep.tile([P, F_TILES, PARAM_ROWS], F32, name="by_filter")
-        nc.vector.tensor_copy(out=by_filter[:], in_=params_ps[:, :, 0:PARAM_ROWS])
-        std = keep.tile([P, F_TILES], F32, name="std")
-        bn_scale = keep.tile([P, F_TILES], F32, name="bn_scale")
-        bn_shift = keep.tile([P, F_TILES, L], F32, name="bn_shift")
-        wide = [P, F_TILES, L]
-        nc.vector.tensor_scalar_add(out=std[:], in0=by_filter[:, :, ROW_VAR], scalar1=BN_EPS)
-        nc.scalar.sqrt(out=std[:], in_=std[:])
-        nc.vector.reciprocal(out=bn_scale[:], in_=std[:])
-        nc.vector.tensor_mul(out=bn_scale[:], in0=bn_scale[:], in1=by_filter[:, :, ROW_GAMMA])
-        nc.vector.scalar_tensor_tensor(
-            out=bn_shift[:],
-            in0=by_filter[:, :, 0:L],
-            scalar=2.0,
-            in1=by_filter[:, :, ROW_MEAN : ROW_MEAN + 1].to_broadcast(wide),
-            op0=ALU.mult,
-            op1=ALU.subtract,
-        )
-        nc.vector.tensor_mul(out=bn_shift[:], in0=bn_shift[:], in1=bn_scale[:].unsqueeze(2).to_broadcast(wide))
-        nc.vector.tensor_add(
-            out=bn_shift[:], in0=bn_shift[:], in1=by_filter[:, :, ROW_BETA : ROW_BETA + 1].to_broadcast(wide)
-        )
+        def batch_norm_by_filter():
+            params_ps = turn_pool.tile([P, TILES, P], BF16, tag="turn")
+            for j in range(TILES):
+                nc.tensor.transpose(params_ps[:, j, :], params[:, P * j : P * (j + 1)], ident_bf16[:])
+            nc.vector.tensor_copy(out=by_filter[:], in_=params_ps[:, :, 0:PARAM_ROWS])
+            wide = [P, TILES, L]
+            nc.vector.tensor_scalar_add(out=std[:], in0=by_filter[:, :, ROW_VAR], scalar1=BN_EPS)
+            nc.scalar.sqrt(out=std[:], in_=std[:])
+            nc.vector.reciprocal(out=bn_scale[:], in_=std[:])
+            nc.vector.tensor_mul(out=bn_scale[:], in0=bn_scale[:], in1=by_filter[:, :, ROW_GAMMA])
+            nc.vector.scalar_tensor_tensor(
+                out=bn_shift[:],
+                in0=by_filter[:, :, 0:L],
+                scalar=2.0,
+                in1=by_filter[:, :, ROW_MEAN : ROW_MEAN + 1].to_broadcast(wide),
+                op0=ALU.mult,
+                op1=ALU.subtract,
+            )
+            nc.vector.tensor_mul(out=bn_shift[:], in0=bn_shift[:], in1=bn_scale[:].unsqueeze(2).to_broadcast(wide))
+            nc.vector.tensor_add(
+                out=bn_shift[:], in0=bn_shift[:], in1=by_filter[:, :, ROW_BETA : ROW_BETA + 1].to_broadcast(wide)
+            )
 
-        def quantise_position(m):
-            words = h_raw[m // 2][:].bitcast(F32)
-            first = (C // 2) * (m % 2)
-            grouped = stage.tile([P, 4 * B], BF16, align_bytes=64)
-            grouped_words = grouped[:].bitcast(F32).rearrange("p (t b u) -> p t b u", t=B_TILES, u=2)
-            for half in range(2):
-                bank = turn_pool.tile([P, 2, 2, P], F32, tag="turn")
-                for s in range(2):
-                    for u in range(2):
-                        nc.tensor.transpose(
-                            bank[:, s, u, :], words[:, 2 * half + s, first + u : first + C // 2 : 2], ident_f32[:]
-                        )
-                copy = nc.scalar.copy if half == 0 else nc.vector.tensor_copy
-                copy(out=grouped_words[:, 2 * half : 2 * half + 2], in_=bank[:].rearrange("p s u b -> p s b u"))
-            nc.vector.quantize_mx(out=h_codes[m][:].bitcast(FP8X4), scales=h_scales[m][:], in_=grouped[:])
+        by_filter = keep.tile([P, TILES, PARAM_ROWS], F32, name="by_filter")
+        std = keep.tile([P, TILES], F32, name="std")
+        bn_scale = keep.tile([P, TILES], F32, name="bn_scale")
+        bn_shift = keep.tile([P, TILES, L], F32, name="bn_shift")
 
-        def multiply(l, j, normed):
+        def repeat(column):
+            squares = ahead.tile([P, TILES, P], F32, name="squares")
+            nc.scalar.copy(out=squares[:], in_=column.to_broadcast([P, TILES, P]))
+            return squares
+
+        def spread(squares, row):
+            bank = turn_pool.tile([P, C], F32, tag="turn")
+            for j in range(TILES):
+                nc.tensor.transpose(bank[:, P * j : P * (j + 1)], squares[:, j, :], ident_f32[:])
+            nc.scalar.copy(out=row, in_=bank[:])
+
+        def quantise_unit(q, t):
+            words = h_raw[q][:, t, :].bitcast(F32)
+            bank = turn_pool.tile([P, 2, 2, P], F32, tag="turn")
+            for e in range(2):
+                for u in range(2):
+                    nc.tensor.transpose(
+                        bank[:, e, u, :], words[:, (C // 2) * e + u : (C // 2) * (e + 1) : 2], ident_f32[:]
+                    )
+            grouped = stage.tile([P, 2, 4 * P], BF16, align_bytes=64)
+            nc.scalar.copy(
+                out=grouped[:].bitcast(F32).rearrange("p e (b u) -> p e b u", u=2),
+                in_=bank[:].rearrange("p e u b -> p e b u"),
+            )
+            for e in range(2):
+                nc.vector.quantize_mx(
+                    out=h_codes[2 * q + e][:, P * t : P * (t + 1)].bitcast(FP8X4),
+                    scales=h_scales[2 * q + e][:, P * t : P * (t + 1)],
+                    in_=grouped[:, e, :],
+                )
+
+        def leaky(values):
+            nc.vector.scalar_tensor_tensor(
+                out=values, in0=values, scalar=LEAKY_ALPHA, in1=values, op0=ALU.mult, op1=ALU.max
+            )
+
+        scale_row = keep.tile([P, C], F32, name="scale_row")
+        x_shifted_of = {}
+        result_of = {}
+
+        def shift_x(l, squares):
+            shift_row = ahead.tile([P, C], F32, name="shift_row")
+            spread(squares, shift_row[:])
+            x_shifted_of[l] = ahead.tile([P, TILES, C], F32, name="x_shifted")
+            for t in range(TILES):
+                nc.gpsimd.tensor_tensor(out=x_shifted_of[l][:, t, :], in0=x_sb[l][:, t, :], in1=shift_row[:], op=ALU.add)
+
+        def batch_products(l, t):
+            acc = acc_pool.tile([P, C], F32, tag="acc")
+            for i in range(TAPS):
+                m = (l - STEP[i]) % L
+                nc.tensor.matmul_mx(
+                    out=acc[:],
+                    lhsT=h_codes[m][:, P * t : P * (t + 1)].bitcast(FP8X4),
+                    lhsT_scale=h_scales[m][:, P * t : P * (t + 1)],
+                    rhs=w_words[l][:, i, :].bitcast(FP4X4),
+                    rhs_scale=w_scales[l][:, i, :],
+                    start=(i == 0),
+                    stop=(i == TAPS - 1),
+                )
+            return acc
+
+        def finish_batch_tile(l, t):
+            leaky(result_of[l][:, t, :])
+            nc.sync.dma_start(out=out_by_l[l][:, t, :], in_=result_of[l][:, t, :])
+
+        normed_of = {}
+
+        def filter_products(l, j):
             acc = acc_pool.tile([P, B], F32, tag="acc")
             for i in range(TAPS):
                 m = (l - STEP[i]) % L
@@ -156,46 +227,63 @@ def tile_residualblock5_pb_t_e_kernel(
                     start=(i == 0),
                     stop=(i == TAPS - 1),
                 )
+            normed_of[l, j] = stage.tile([P, B], F32, name="normed")
             nc.scalar.activation(
-                out=normed[:, j, :],
+                out=normed_of[l, j][:],
                 in_=acc[:],
                 func=ACT.Identity,
                 bias=bn_shift[:, j, l : l + 1],
                 scale=bn_scale[:, j : j + 1],
             )
 
-        def finish(l, normed):
-            result = out_pool.tile([P, B_TILES, C], F32)
-            x_l = x_sb[l // 2][:, :, C * (l % 2) : C * (l % 2 + 1)]
-            for half in range(2):
-                pair = slice(2 * half, 2 * half + 2)
-                for t in range(2 * half, 2 * half + 2):
-                    bank = turn_pool.tile([P, C], F32, tag="turn")
-                    for j in range(F_TILES):
-                        nc.tensor.transpose(
-                            bank[:, P * j : P * (j + 1)], normed[:, j, P * t : P * (t + 1)], ident_f32[:]
-                        )
-                    nc.vector.tensor_tensor(out=result[:, t, :], in0=bank[:], in1=x_l[:, t, :], op=ALU.add)
-                nc.vector.scalar_tensor_tensor(
-                    out=result[:, pair, :],
-                    in0=result[:, pair, :],
-                    scalar=LEAKY_ALPHA,
-                    in1=result[:, pair, :],
-                    op0=ALU.mult,
-                    op1=ALU.max,
-                )
-                nc.sync.dma_start(out=out_by_l[l][:, pair, :], in_=result[:, pair, :])
+        def turn_back(l, j):
+            if j == 0:
+                result_of[l] = out_pool.tile([P, TILES, C], F32, name="result")
+            bank = turn_pool.tile([P, TILES, P], F32, tag="turn")
+            for t in range(TILES):
+                nc.tensor.transpose(bank[:, t, :], normed_of[l, j][:, P * t : P * (t + 1)], ident_f32[:])
+            cols = slice(P * j, P * (j + 1))
+            nc.vector.tensor_tensor(out=result_of[l][:, :, cols], in0=bank[:], in1=x_sb[l][:, :, cols], op=ALU.add)
 
-        for m in (0, 1, 6, 7):
-            quantise_position(m)
-        normed_of = {}
-        for l in range(L):
-            normed_of[l] = norm_pool.tile([P, F_TILES, B], F32, name="normed")
-            for j in range(F_TILES):
-                multiply(l, j, normed_of[l])
-                if j == 0:
-                    if 2 <= l + 2 <= 5:
-                        quantise_position(l + 2)
-                    if l >= 1:
-                        finish(l - 1, normed_of[l - 1])
-        finish(L - 1, normed_of[L - 1])
+        def finish_filter_tile(l, j):
+            cols = slice(P * j, P * (j + 1))
+            leaky(result_of[l][:, :, cols])
+            nc.sync.dma_start(out=out_by_l[l][:, :, cols], in_=result_of[l][:, :, cols])
+
+        for q, t in UNITS[:UNITS_AHEAD]:
+            quantise_unit(q, t)
+        batch_norm_by_filter()
+        scale_squares = repeat(bn_scale[:].unsqueeze(2))
+        shift_squares = repeat(bn_shift[:, :, 0:1])
+
+        for s in range(len(BATCH_GROUPS)):
+            l, t = BATCH_GROUPS[s]
+            l_next = BATCH_MAJOR[s // TILES + 1] if s // TILES + 1 < len(BATCH_MAJOR) else None
+            filter_group = FILTER_GROUPS[s - LAG] if s >= LAG else None
+            if t == 0:
+                result_of[l] = out_pool.tile([P, TILES, C], F32, name="result")
+            if filter_group is not None:
+                filter_products(*filter_group)
+            acc = batch_products(l, t)
+            if s == 0:
+                spread(scale_squares, scale_row[:])
+                shift_x(l, shift_squares)
+            nc.vector.tensor_tensor(out=result_of[l][:, t, :], in0=acc[:], in1=scale_row[:], op=ALU.mult)
+            if s >= 1:
+                finish_batch_tile(*BATCH_GROUPS[s - 1])
+            nc.vector.tensor_tensor(
+                out=result_of[l][:, t, :], in0=result_of[l][:, t, :], in1=x_shifted_of[l][:, t, :], op=ALU.add
+            )
+            if filter_group is not None:
+                turn_back(*filter_group)
+            if s - 1 >= LAG:
+                finish_filter_tile(*FILTER_GROUPS[s - 1 - LAG])
+            done = UNITS_AHEAD + UNITS_PER_STEP * s
+            for q, tile_of_unit in UNITS[done : done + UNITS_PER_STEP]:
+                quantise_unit(q, tile_of_unit)
+            if t == 1 and l_next is not None:
+                shift_squares = repeat(bn_shift[:, :, l_next : l_next + 1])
+            if t == 2 and l_next is not None:
+                shift_x(l_next, shift_squares)
+        finish_filter_tile(*FILTER_GROUPS[-1])
+        finish_batch_tile(*BATCH_GROUPS[-1])

@@ -28,6 +28,8 @@ FILTER_MAJOR = (1, 3, 5)
 LAG = TILES * (len(BATCH_MAJOR) - len(FILTER_MAJOR))
 BATCH_GROUPS = [(l, t) for l in BATCH_MAJOR for t in range(TILES)]
 FILTER_GROUPS = [(l, j) for l in FILTER_MAJOR for j in range(TILES)]
+BATCH_HALVES = [(l, half) for l in BATCH_MAJOR for half in range(2)]
+FILTER_HALVES = [(l, half) for l in FILTER_MAJOR for half in range(2)]
 
 UNITS = [(q, t) for t in range(TILES) for q in (0, 3)] + [(q, t) for q in (1, 2) for t in range(TILES)]
 UNITS_AHEAD = 4
@@ -94,11 +96,11 @@ def tile_residualblock5_pb_t_e_kernel(
             nc.sync.dma_start(out=w_words[l][:].bitcast(I32), in_=words_by_l[l])
 
         def load_params():
-            nc.scalar.dma_start(out=params[0:L, :], in_=b2)
-            nc.scalar.dma_start(out=params[ROW_GAMMA : ROW_GAMMA + 1, :], in_=gamma2.unsqueeze(0))
-            nc.scalar.dma_start(out=params[ROW_BETA : ROW_BETA + 1, :], in_=beta2.unsqueeze(0))
-            nc.scalar.dma_start(out=params[ROW_MEAN : ROW_MEAN + 1, :], in_=mean2.unsqueeze(0))
-            nc.scalar.dma_start(out=params[ROW_VAR : ROW_VAR + 1, :], in_=var2.unsqueeze(0))
+            nc.sync.dma_start(out=params[0:L, :], in_=b2)
+            nc.sync.dma_start(out=params[ROW_GAMMA : ROW_GAMMA + 1, :], in_=gamma2.unsqueeze(0))
+            nc.sync.dma_start(out=params[ROW_BETA : ROW_BETA + 1, :], in_=beta2.unsqueeze(0))
+            nc.sync.dma_start(out=params[ROW_MEAN : ROW_MEAN + 1, :], in_=mean2.unsqueeze(0))
+            nc.sync.dma_start(out=params[ROW_VAR : ROW_VAR + 1, :], in_=var2.unsqueeze(0))
 
         load_h_ends(0)
         load_h_ends(1)
@@ -208,9 +210,16 @@ def tile_residualblock5_pb_t_e_kernel(
                 )
             return acc
 
-        def finish_batch_tile(l, t):
-            leaky(result_of[l][:, t, :])
-            nc.sync.dma_start(out=out_by_l[l][:, t, :], in_=result_of[l][:, t, :])
+        def add_x(l, half):
+            tiles = slice(2 * half, 2 * half + 2)
+            nc.vector.tensor_tensor(
+                out=result_of[l][:, tiles, :], in0=result_of[l][:, tiles, :], in1=x_shifted_of[l][:, tiles, :], op=ALU.add
+            )
+
+        def finish_batch_half(l, half):
+            tiles = slice(2 * half, 2 * half + 2)
+            leaky(result_of[l][:, tiles, :])
+            nc.sync.dma_start(out=out_by_l[l][:, tiles, :], in_=result_of[l][:, tiles, :])
 
         normed_of = {}
 
@@ -245,8 +254,8 @@ def tile_residualblock5_pb_t_e_kernel(
             cols = slice(P * j, P * (j + 1))
             nc.vector.tensor_tensor(out=result_of[l][:, :, cols], in0=bank[:], in1=x_sb[l][:, :, cols], op=ALU.add)
 
-        def finish_filter_tile(l, j):
-            cols = slice(P * j, P * (j + 1))
+        def finish_filter_half(l, half):
+            cols = slice(2 * P * half, 2 * P * (half + 1))
             leaky(result_of[l][:, :, cols])
             nc.sync.dma_start(out=out_by_l[l][:, :, cols], in_=result_of[l][:, :, cols])
 
@@ -268,16 +277,15 @@ def tile_residualblock5_pb_t_e_kernel(
             if s == 0:
                 spread(scale_squares, scale_row[:])
                 shift_x(l, shift_squares)
+            if s % 2 == 0 and s - LAG >= 2:
+                finish_filter_half(*FILTER_HALVES[(s - LAG) // 2 - 1])
+            if s % 2 == 1 and s >= 3:
+                finish_batch_half(*BATCH_HALVES[s // 2 - 1])
             nc.vector.tensor_tensor(out=result_of[l][:, t, :], in0=acc[:], in1=scale_row[:], op=ALU.mult)
-            if s >= 1:
-                finish_batch_tile(*BATCH_GROUPS[s - 1])
-            nc.vector.tensor_tensor(
-                out=result_of[l][:, t, :], in0=result_of[l][:, t, :], in1=x_shifted_of[l][:, t, :], op=ALU.add
-            )
             if filter_group is not None:
                 turn_back(*filter_group)
-            if s - 1 >= LAG:
-                finish_filter_tile(*FILTER_GROUPS[s - 1 - LAG])
+            if s % 2 == 1:
+                add_x(*BATCH_HALVES[s // 2])
             done = UNITS_AHEAD + UNITS_PER_STEP * s
             for q, tile_of_unit in UNITS[done : done + UNITS_PER_STEP]:
                 quantise_unit(q, tile_of_unit)
@@ -285,5 +293,5 @@ def tile_residualblock5_pb_t_e_kernel(
                 shift_squares = repeat(bn_shift[:, :, l_next : l_next + 1])
             if t == 2 and l_next is not None:
                 shift_x(l_next, shift_squares)
-        finish_filter_tile(*FILTER_GROUPS[-1])
-        finish_batch_tile(*BATCH_GROUPS[-1])
+        finish_filter_half(*FILTER_HALVES[-1])
+        finish_batch_half(*BATCH_HALVES[-1])

@@ -19,17 +19,13 @@ L = 8
 C = 512
 TAPS = 5
 STEP = (0, 0, 1, -1, 2)
+TAP_ORDER = (0, 1, 2, 4, 3)
 BN_EPS = 1e-3
 LEAKY_ALPHA = 0.3
 TILES = 4
 
-BATCH_MAJOR = (0, 2, 4, 6, 7)
-FILTER_MAJOR = (1, 3, 5)
-LAG = TILES * (len(BATCH_MAJOR) - len(FILTER_MAJOR))
-BATCH_GROUPS = [(l, t) for l in BATCH_MAJOR for t in range(TILES)]
-FILTER_GROUPS = [(l, j) for l in FILTER_MAJOR for j in range(TILES)]
-BATCH_HALVES = [(l, half) for l in BATCH_MAJOR for half in range(2)]
-FILTER_HALVES = [(l, half) for l in FILTER_MAJOR for half in range(2)]
+BATCH_MAJOR = (0, 3, 5)
+GROUPS = [(l, k) for l in range(L) for k in range(TILES)]
 
 UNITS = [(q, t) for t in range(TILES) for q in (0, 3)] + [(q, t) for q in (1, 2) for t in range(TILES)]
 UNITS_AHEAD = 4
@@ -38,6 +34,15 @@ UNITS_PER_STEP = 2
 FLOPS = 2 * B * L * TAPS * C * C
 
 ROW_GAMMA, ROW_BETA, ROW_MEAN, ROW_VAR, PARAM_ROWS = L, L + 1, L + 2, L + 3, L + 4
+
+
+def turns_after(s):
+    l, k = GROUPS[s]
+    if l == L - 1 and k >= 2:
+        return [(l, 0), (l, 1)] if k == 2 else [(l, 2)]
+    if k == 0 and l >= 1 and l - 1 not in BATCH_MAJOR:
+        return [(l - 1, j) for j in range(TILES)]
+    return []
 
 
 def tile_residualblock5_pb_t_e_kernel(
@@ -55,8 +60,9 @@ def tile_residualblock5_pb_t_e_kernel(
         ctx.enter_context(tc.manual_schedule())
         keep = ctx.enter_context(tc.tile_pool(name="keep", bufs=1))
         stage = ctx.enter_context(tc.tile_pool(name="stage", bufs=3))
+        normed_pool = ctx.enter_context(tc.tile_pool(name="normed", bufs=6))
         ahead = ctx.enter_context(tc.tile_pool(name="ahead", bufs=2))
-        out_pool = ctx.enter_context(tc.tile_pool(name="outs", bufs=5))
+        out_pool = ctx.enter_context(tc.tile_pool(name="outs", bufs=4))
         acc_pool = ctx.enter_context(tc.psum_pool(name="acc", bufs=4))
         turn_pool = ctx.enter_context(tc.psum_pool(name="turn", bufs=4))
 
@@ -84,8 +90,9 @@ def tile_residualblock5_pb_t_e_kernel(
         def load_h_ends(t):
             nc.sync.dma_start(out=h_ends[:, t], in_=h_pairs[:, t, 0:4:3, :])
 
-        def load_h_mid(q):
-            nc.sync.dma_start(out=h_mid[:, q - 1], in_=h_pairs[:, :, q, :])
+        def load_h_mid(q, half):
+            tiles = slice(2 * half, 2 * half + 2)
+            nc.sync.dma_start(out=h_mid[:, q - 1, tiles], in_=h_pairs[:, tiles, q, :])
 
         def load_x(l):
             nc.sync.dma_start(out=x_sb[l][:], in_=x_by_l[l])
@@ -102,23 +109,31 @@ def tile_residualblock5_pb_t_e_kernel(
             nc.sync.dma_start(out=params[ROW_MEAN : ROW_MEAN + 1, :], in_=mean2.unsqueeze(0))
             nc.sync.dma_start(out=params[ROW_VAR : ROW_VAR + 1, :], in_=var2.unsqueeze(0))
 
+        load_params()
         load_h_ends(0)
         load_h_ends(1)
         load_weights(0)
-        load_params()
         nc.scalar.sqrt(out=one[:], in_=one[:])
         load_h_ends(2)
-        load_x(0)
         load_h_ends(3)
-        load_h_mid(1)
-        load_x(2)
+        load_x(0)
+        load_h_mid(1, 0)
+        load_h_mid(1, 1)
+        load_weights(1)
+        load_h_mid(2, 0)
+        load_h_mid(2, 1)
         load_weights(2)
-        load_h_mid(2)
-        for l_batch, l_filter in zip(BATCH_MAJOR[2:], FILTER_MAJOR):
-            load_x(l_batch)
-            load_weights(l_batch)
-            load_weights(l_filter)
-            load_x(l_filter)
+        load_x(1)
+        load_x(3)
+        load_weights(3)
+        load_x(2)
+        load_weights(4)
+        load_x(5)
+        load_x(4)
+        for l in range(5, L):
+            load_weights(l)
+            if l > 5:
+                load_x(l)
 
         def batch_norm_by_filter():
             params_ps = turn_pool.tile([P, TILES, P], BF16, tag="turn")
@@ -159,7 +174,7 @@ def tile_residualblock5_pb_t_e_kernel(
                 nc.tensor.transpose(bank[:, P * j : P * (j + 1)], squares[:, j, :], ident_f32[:])
             nc.scalar.copy(out=row, in_=bank[:])
 
-        def quantise_unit(q, t):
+        def turn_unit(q, t):
             words = h_raw[q][:, t, :].bitcast(F32)
             bank = turn_pool.tile([P, 2, 2, P], F32, tag="turn")
             for e in range(2):
@@ -167,11 +182,14 @@ def tile_residualblock5_pb_t_e_kernel(
                     nc.tensor.transpose(
                         bank[:, e, u, :], words[:, (C // 2) * e + u : (C // 2) * (e + 1) : 2], ident_f32[:]
                     )
-            grouped = stage.tile([P, 2, 4 * P], BF16, align_bytes=64)
+            grouped = stage.tile([P, 2, 4 * P], BF16, name="grouped", align_bytes=64)
             nc.scalar.copy(
                 out=grouped[:].bitcast(F32).rearrange("p e (b u) -> p e b u", u=2),
                 in_=bank[:].rearrange("p e u b -> p e b u"),
             )
+            return grouped
+
+        def quantise_unit(q, t, grouped):
             for e in range(2):
                 nc.vector.quantize_mx(
                     out=h_codes[2 * q + e][:, P * t : P * (t + 1)].bitcast(FP8X4),
@@ -185,19 +203,24 @@ def tile_residualblock5_pb_t_e_kernel(
             )
 
         scale_row = keep.tile([P, C], F32, name="scale_row")
-        x_shifted_of = {}
+        shift_row = {}
+        for l in BATCH_MAJOR:
+            shift_row[l] = keep.tile([P, C], F32, name="shift_row%d" % l)
+        x_shifted = keep.tile([P, TILES, C], F32, name="x_shifted")
         result_of = {}
 
-        def shift_x(l, squares):
-            shift_row = ahead.tile([P, C], F32, name="shift_row")
-            spread(squares, shift_row[:])
-            x_shifted_of[l] = ahead.tile([P, TILES, C], F32, name="x_shifted")
-            for t in range(TILES):
-                nc.gpsimd.tensor_tensor(out=x_shifted_of[l][:, t, :], in0=x_sb[l][:, t, :], in1=shift_row[:], op=ALU.add)
+        def shift_x(l, half):
+            tiles = slice(2 * half, 2 * half + 2)
+            nc.vector.tensor_tensor(
+                out=x_shifted[:, tiles, :],
+                in0=x_sb[l][:, tiles, :],
+                in1=shift_row[l][:].unsqueeze(1).to_broadcast([P, 2, C]),
+                op=ALU.add,
+            )
 
         def batch_products(l, t):
             acc = acc_pool.tile([P, C], F32, tag="acc")
-            for i in range(TAPS):
+            for i in TAP_ORDER:
                 m = (l - STEP[i]) % L
                 nc.tensor.matmul_mx(
                     out=acc[:],
@@ -205,15 +228,15 @@ def tile_residualblock5_pb_t_e_kernel(
                     lhsT_scale=h_scales[m][:, P * t : P * (t + 1)],
                     rhs=w_words[l][:, i, :].bitcast(FP4X4),
                     rhs_scale=w_scales[l][:, i, :],
-                    start=(i == 0),
-                    stop=(i == TAPS - 1),
+                    start=(i == TAP_ORDER[0]),
+                    stop=(i == TAP_ORDER[-1]),
                 )
             return acc
 
         def add_x(l, half):
             tiles = slice(2 * half, 2 * half + 2)
             nc.vector.tensor_tensor(
-                out=result_of[l][:, tiles, :], in0=result_of[l][:, tiles, :], in1=x_shifted_of[l][:, tiles, :], op=ALU.add
+                out=result_of[l][:, tiles, :], in0=result_of[l][:, tiles, :], in1=x_shifted[:, tiles, :], op=ALU.add
             )
 
         def finish_batch_half(l, half):
@@ -225,7 +248,7 @@ def tile_residualblock5_pb_t_e_kernel(
 
         def filter_products(l, j):
             acc = acc_pool.tile([P, B], F32, tag="acc")
-            for i in range(TAPS):
+            for i in TAP_ORDER:
                 m = (l - STEP[i]) % L
                 nc.tensor.matmul_mx(
                     out=acc[:],
@@ -233,10 +256,10 @@ def tile_residualblock5_pb_t_e_kernel(
                     lhsT_scale=w_scales[l][:, i, P * j : P * (j + 1)],
                     rhs=h_codes[m][:].bitcast(FP8X4),
                     rhs_scale=h_scales[m][:],
-                    start=(i == 0),
-                    stop=(i == TAPS - 1),
+                    start=(i == TAP_ORDER[0]),
+                    stop=(i == TAP_ORDER[-1]),
                 )
-            normed_of[l, j] = stage.tile([P, B], F32, name="normed")
+            normed_of[l, j] = normed_pool.tile([P, B], F32, name="normed")
             nc.scalar.activation(
                 out=normed_of[l, j][:],
                 in_=acc[:],
@@ -259,39 +282,49 @@ def tile_residualblock5_pb_t_e_kernel(
             leaky(result_of[l][:, :, cols])
             nc.sync.dma_start(out=out_by_l[l][:, :, cols], in_=result_of[l][:, :, cols])
 
-        for q, t in UNITS[:UNITS_AHEAD]:
-            quantise_unit(q, t)
         batch_norm_by_filter()
-        scale_squares = repeat(bn_scale[:].unsqueeze(2))
-        shift_squares = repeat(bn_shift[:, :, 0:1])
+        for q, t in UNITS[:UNITS_AHEAD]:
+            quantise_unit(q, t, turn_unit(q, t))
+        rows = [(bn_scale[:].unsqueeze(2), scale_row)] + [(bn_shift[:, :, l : l + 1], shift_row[l]) for l in BATCH_MAJOR]
+        squares_of = {0: repeat(rows[0][0]), 1: repeat(rows[1][0])}
 
-        for s in range(len(BATCH_GROUPS)):
-            l, t = BATCH_GROUPS[s]
-            l_next = BATCH_MAJOR[s // TILES + 1] if s // TILES + 1 < len(BATCH_MAJOR) else None
-            filter_group = FILTER_GROUPS[s - LAG] if s >= LAG else None
-            if t == 0:
-                result_of[l] = out_pool.tile([P, TILES, C], F32, name="result")
-            if filter_group is not None:
-                filter_products(*filter_group)
-            acc = batch_products(l, t)
-            if s == 0:
-                spread(scale_squares, scale_row[:])
-                shift_x(l, shift_squares)
-            if s % 2 == 0 and s - LAG >= 2:
-                finish_filter_half(*FILTER_HALVES[(s - LAG) // 2 - 1])
-            if s % 2 == 1 and s >= 3:
-                finish_batch_half(*BATCH_HALVES[s // 2 - 1])
-            nc.vector.tensor_tensor(out=result_of[l][:, t, :], in0=acc[:], in1=scale_row[:], op=ALU.mult)
-            if filter_group is not None:
-                turn_back(*filter_group)
-            if s % 2 == 1:
-                add_x(*BATCH_HALVES[s // 2])
+        waiting = []
+
+        for s in range(len(GROUPS)):
+            l, k = GROUPS[s]
+            batch = l in BATCH_MAJOR
+            turns = turns_after(s)
+            for item in waiting[: (1 if batch or turns else 2)]:
+                item[0](item[1], item[2])
+                waiting.remove(item)
+            if batch:
+                if k == 0:
+                    result_of[l] = out_pool.tile([P, TILES, C], F32, name="result")
+                acc = batch_products(l, k)
+                if s == 0:
+                    spread(squares_of[0], rows[0][1][:])
+                    spread(squares_of[1], rows[1][1][:])
+                nc.vector.tensor_tensor(out=result_of[l][:, k, :], in0=acc[:], in1=scale_row[:], op=ALU.mult)
+                if k % 2 == 1:
+                    waiting.extend([(add_x, l, k // 2), (finish_batch_half, l, k // 2)])
+            else:
+                filter_products(l, k)
+            for l_turn, j in turns:
+                turn_back(l_turn, j)
+                if j % 2 == 1:
+                    waiting.append((finish_filter_half, l_turn, j // 2))
+            if 1 <= s < len(rows) - 1:
+                spread(squares_of[s + 1], rows[s + 1][1][:])
+            if s + 2 < len(rows):
+                squares_of[s + 2] = repeat(rows[s + 2][0])
             done = UNITS_AHEAD + UNITS_PER_STEP * s
-            for q, tile_of_unit in UNITS[done : done + UNITS_PER_STEP]:
-                quantise_unit(q, tile_of_unit)
-            if t == 1 and l_next is not None:
-                shift_squares = repeat(bn_shift[:, :, l_next : l_next + 1])
-            if t == 2 and l_next is not None:
-                shift_x(l_next, shift_squares)
-        finish_filter_half(*FILTER_HALVES[-1])
-        finish_batch_half(*BATCH_HALVES[-1])
+            units = [(q, t, turn_unit(q, t)) for q, t in UNITS[done : done + UNITS_PER_STEP]]
+            for q, t, grouped in units:
+                quantise_unit(q, t, grouped)
+            if k == 0 and (l + 1 in BATCH_MAJOR or s == 0):
+                l_next = l if s == 0 else l + 1
+                waiting.extend([(shift_x, l_next, 0), (shift_x, l_next, 1)])
+        turn_back(L - 1, TILES - 1)
+        waiting.append((finish_filter_half, L - 1, 1))
+        for item in waiting:
+            item[0](item[1], item[2])

@@ -30,6 +30,7 @@ GROUPS = [(l, k) for l in range(L) for k in range(TILES)]
 UNITS = [(q, t) for t in range(TILES) for q in (0, 3)] + [(q, t) for q in (1, 2) for t in range(TILES)]
 UNITS_AHEAD = 4
 UNITS_PER_STEP = 2
+HOLD = 4
 
 FLOPS = 2 * B * L * TAPS * C * C
 
@@ -51,7 +52,7 @@ def tile_residualblock5_pb_t_e_kernel(
     nc = tc.nc
 
     h_pairs = h.rearrange("(t p) (q e) c -> p t q (e c)", p=P, e=2)
-    x_by_l = x.rearrange("(t p) l f -> l p t f", p=P)
+    x_quads = x.rearrange("(t p) (g e) f -> g p t (e f)", p=P, e=4)
     out_by_l = out.rearrange("(t p) l f -> l p t f", p=P)
     words_by_l = k2_words.bitcast(I32).rearrange("(i l) p w -> l p i w", l=L)
     scales_by_l = k2_scales.bitcast(I32).rearrange("(i l) (q r) n -> l r q i n", l=L, r=4)
@@ -72,7 +73,8 @@ def tile_residualblock5_pb_t_e_kernel(
         h_ends = keep.tile([P, TILES, 2, 2 * C], BF16, name="h_ends")
         h_mid = keep.tile([P, 2, TILES, 2 * C], BF16, name="h_mid")
         h_raw = {0: h_ends[:, :, 0, :], 1: h_mid[:, 0], 2: h_mid[:, 1], 3: h_ends[:, :, 1, :]}
-        x_sb = [keep.tile([P, TILES, C], BF16, name="x_sb%d" % l) for l in range(L)]
+        x_half = [keep.tile([P, TILES, 4, C], BF16, name="x_half%d" % g) for g in range(2)]
+        x_sb = [x_half[l // 4][:, :, l % 4, :] for l in range(L)]
         w_words = [keep.tile([P, TAPS, 2 * C], U8, name="w_words%d" % l, align_bytes=64) for l in range(L)]
         w_scales = [keep.tile([P, TAPS, C], U8, name="w_scales%d" % l, align_bytes=64) for l in range(L)]
         h_codes = [keep.tile([P, B], U32, name="h_codes%d" % m, align_bytes=64) for m in range(L)]
@@ -94,8 +96,9 @@ def tile_residualblock5_pb_t_e_kernel(
             tiles = slice(2 * half, 2 * half + 2)
             nc.sync.dma_start(out=h_mid[:, q - 1, tiles], in_=h_pairs[:, tiles, q, :])
 
-        def load_x(l):
-            nc.sync.dma_start(out=x_sb[l][:], in_=x_by_l[l])
+        def load_x(g, half):
+            tiles = slice(2 * half, 2 * half + 2)
+            nc.sync.dma_start(out=x_half[g][:, tiles].rearrange("p t e f -> p t (e f)"), in_=x_quads[g][:, tiles, :])
 
         def load_weights(l):
             for r in range(4):
@@ -116,24 +119,19 @@ def tile_residualblock5_pb_t_e_kernel(
         nc.scalar.sqrt(out=one[:], in_=one[:])
         load_h_ends(2)
         load_h_ends(3)
-        load_x(0)
         load_h_mid(1, 0)
         load_h_mid(1, 1)
         load_weights(1)
+        load_x(0, 0)
+        load_x(0, 1)
         load_h_mid(2, 0)
         load_h_mid(2, 1)
         load_weights(2)
-        load_x(1)
-        load_x(3)
         load_weights(3)
-        load_x(2)
-        load_weights(4)
-        load_x(5)
-        load_x(4)
-        for l in range(5, L):
+        load_x(1, 0)
+        load_x(1, 1)
+        for l in range(4, L):
             load_weights(l)
-            if l > 5:
-                load_x(l)
 
         def batch_norm_by_filter():
             params_ps = turn_pool.tile([P, TILES, P], BF16, tag="turn")
@@ -239,7 +237,7 @@ def tile_residualblock5_pb_t_e_kernel(
                 out=result_of[l][:, tiles, :], in0=result_of[l][:, tiles, :], in1=x_shifted[:, tiles, :], op=ALU.add
             )
 
-        def finish_batch_half(l, half):
+        def finish_half(l, half):
             tiles = slice(2 * half, 2 * half + 2)
             leaky(result_of[l][:, tiles, :])
             nc.sync.dma_start(out=out_by_l[l][:, tiles, :], in_=result_of[l][:, tiles, :])
@@ -277,6 +275,14 @@ def tile_residualblock5_pb_t_e_kernel(
             cols = slice(P * j, P * (j + 1))
             nc.vector.tensor_tensor(out=result_of[l][:, :, cols], in0=bank[:], in1=x_sb[l][:, :, cols], op=ALU.add)
 
+        def turn_back_tile(l, t):
+            if t == 0:
+                result_of[l] = out_pool.tile([P, TILES, C], F32, name="result")
+            bank = turn_pool.tile([P, C], F32, tag="turn")
+            for j in range(TILES):
+                nc.tensor.transpose(bank[:, P * j : P * (j + 1)], normed_of[l, j][:, P * t : P * (t + 1)], ident_f32[:])
+            nc.vector.tensor_tensor(out=result_of[l][:, t, :], in0=bank[:], in1=x_sb[l][:, t, :], op=ALU.add)
+
         def finish_filter_half(l, half):
             cols = slice(2 * P * half, 2 * P * (half + 1))
             leaky(result_of[l][:, :, cols])
@@ -289,11 +295,14 @@ def tile_residualblock5_pb_t_e_kernel(
         squares_of = {0: repeat(rows[0][0]), 1: repeat(rows[1][0])}
 
         waiting = []
+        held = []
 
         for s in range(len(GROUPS)):
             l, k = GROUPS[s]
             batch = l in BATCH_MAJOR
             turns = turns_after(s)
+            if s == HOLD:
+                waiting.extend(held)
             for item in waiting[: (1 if batch or turns else 2)]:
                 item[0](item[1], item[2])
                 waiting.remove(item)
@@ -306,13 +315,18 @@ def tile_residualblock5_pb_t_e_kernel(
                     spread(squares_of[1], rows[1][1][:])
                 nc.vector.tensor_tensor(out=result_of[l][:, k, :], in0=acc[:], in1=scale_row[:], op=ALU.mult)
                 if k % 2 == 1:
-                    waiting.extend([(add_x, l, k // 2), (finish_batch_half, l, k // 2)])
+                    (held if s < HOLD else waiting).extend([(add_x, l, k // 2), (finish_half, l, k // 2)])
             else:
                 filter_products(l, k)
             for l_turn, j in turns:
-                turn_back(l_turn, j)
-                if j % 2 == 1:
-                    waiting.append((finish_filter_half, l_turn, j // 2))
+                if l_turn < L - 1:
+                    turn_back_tile(l_turn, j)
+                    if j % 2 == 1:
+                        waiting.append((finish_half, l_turn, j // 2))
+                else:
+                    turn_back(l_turn, j)
+                    if j % 2 == 1:
+                        waiting.append((finish_filter_half, l_turn, j // 2))
             if 1 <= s < len(rows) - 1:
                 spread(squares_of[s + 1], rows[s + 1][1][:])
             if s + 2 < len(rows):
@@ -323,7 +337,7 @@ def tile_residualblock5_pb_t_e_kernel(
                 quantise_unit(q, t, grouped)
             if k == 0 and (l + 1 in BATCH_MAJOR or s == 0):
                 l_next = l if s == 0 else l + 1
-                waiting.extend([(shift_x, l_next, 0), (shift_x, l_next, 1)])
+                (held if s < HOLD else waiting).extend([(shift_x, l_next, 0), (shift_x, l_next, 1)])
         turn_back(L - 1, TILES - 1)
         waiting.append((finish_filter_half, L - 1, 1))
         for item in waiting:

@@ -30,6 +30,9 @@ GROUPS = [(l, k) for l in range(L) for k in range(TILES)]
 UNITS = [(q, t) for t in range(TILES) for q in (0, 3)] + [(q, t) for q in (1, 2) for t in range(TILES)]
 UNITS_AHEAD = 4
 UNITS_PER_STEP = 2
+STEP_OF_UNIT = {
+    n: (n - UNITS_AHEAD) // UNITS_PER_STEP + (2 if n >= len(UNITS) - TILES else 0) for n in range(UNITS_AHEAD, len(UNITS))
+}
 HOLD = 4
 
 FLOPS = 2 * B * L * TAPS * C * C
@@ -40,7 +43,7 @@ ROW_GAMMA, ROW_BETA, ROW_MEAN, ROW_VAR, PARAM_ROWS = L, L + 1, L + 2, L + 3, L +
 def turns_after(s):
     l, k = GROUPS[s]
     if l == L - 1 and k >= 2:
-        return [(l, 0), (l, 1)] if k == 2 else [(l, 2)]
+        return [(l, 0), (l, 1)] if k == 2 else []
     if k == 0 and l >= 1 and l - 1 not in BATCH_MAJOR:
         return [(l - 1, j) for j in range(TILES)]
     return []
@@ -62,6 +65,7 @@ def tile_residualblock5_pb_t_e_kernel(
         keep = ctx.enter_context(tc.tile_pool(name="keep", bufs=1))
         stage = ctx.enter_context(tc.tile_pool(name="stage", bufs=3))
         normed_pool = ctx.enter_context(tc.tile_pool(name="normed", bufs=6))
+        sort_pool = ctx.enter_context(tc.tile_pool(name="sort", bufs=2 * UNITS_PER_STEP + 1))
         ahead = ctx.enter_context(tc.tile_pool(name="ahead", bufs=2))
         out_pool = ctx.enter_context(tc.tile_pool(name="outs", bufs=4))
         acc_pool = ctx.enter_context(tc.psum_pool(name="acc", bufs=4))
@@ -172,14 +176,25 @@ def tile_residualblock5_pb_t_e_kernel(
                 nc.tensor.transpose(bank[:, P * j : P * (j + 1)], squares[:, j, :], ident_f32[:])
             nc.scalar.copy(out=row, in_=bank[:])
 
+        sorted_of = {}
+
+        def sort_unit(q, t):
+            sorted_of[q, t] = sort_pool.tile([P, 2, 2, P], F32, name="sorted_words")
+            nc.vector.tensor_copy(
+                out=sorted_of[q, t][:], in_=h_raw[q][:, t, :].bitcast(F32).rearrange("p (e w u) -> p e u w", e=2, u=2)
+            )
+
         def turn_unit(q, t):
             words = h_raw[q][:, t, :].bitcast(F32)
             bank = turn_pool.tile([P, 2, 2, P], F32, tag="turn")
             for e in range(2):
                 for u in range(2):
-                    nc.tensor.transpose(
-                        bank[:, e, u, :], words[:, (C // 2) * e + u : (C // 2) * (e + 1) : 2], ident_f32[:]
-                    )
+                    if (q, t) in sorted_of:
+                        nc.tensor.transpose(bank[:, e, u, :], sorted_of[q, t][:, e, u, :], ident_f32[:])
+                    else:
+                        nc.tensor.transpose(
+                            bank[:, e, u, :], words[:, (C // 2) * e + u : (C // 2) * (e + 1) : 2], ident_f32[:]
+                        )
             grouped = stage.tile([P, 2, 4 * P], BF16, name="grouped", align_bytes=64)
             nc.scalar.copy(
                 out=grouped[:].bitcast(F32).rearrange("p e (b u) -> p e b u", u=2),
@@ -244,9 +259,11 @@ def tile_residualblock5_pb_t_e_kernel(
 
         normed_of = {}
 
-        def filter_products(l, j):
+        def filter_products(l, j, interlude=None, pieces=1):
             acc = acc_pool.tile([P, B], F32, tag="acc")
             for i in TAP_ORDER:
+                if interlude is not None and i == TAP_ORDER[3]:
+                    interlude()
                 m = (l - STEP[i]) % L
                 nc.tensor.matmul_mx(
                     out=acc[:],
@@ -258,13 +275,15 @@ def tile_residualblock5_pb_t_e_kernel(
                     stop=(i == TAP_ORDER[-1]),
                 )
             normed_of[l, j] = normed_pool.tile([P, B], F32, name="normed")
-            nc.scalar.activation(
-                out=normed_of[l, j][:],
-                in_=acc[:],
-                func=ACT.Identity,
-                bias=bn_shift[:, j, l : l + 1],
-                scale=bn_scale[:, j : j + 1],
-            )
+            for piece in range(pieces):
+                span = slice(B // pieces * piece, B // pieces * (piece + 1))
+                nc.scalar.activation(
+                    out=normed_of[l, j][:, span],
+                    in_=acc[:, span],
+                    func=ACT.Identity,
+                    bias=bn_shift[:, j, l : l + 1],
+                    scale=bn_scale[:, j : j + 1],
+                )
 
         def turn_back(l, j):
             if j == 0:
@@ -283,14 +302,19 @@ def tile_residualblock5_pb_t_e_kernel(
                 nc.tensor.transpose(bank[:, P * j : P * (j + 1)], normed_of[l, j][:, P * t : P * (t + 1)], ident_f32[:])
             nc.vector.tensor_tensor(out=result_of[l][:, t, :], in0=bank[:], in1=x_sb[l][:, t, :], op=ALU.add)
 
+        def finish_filter_cols(l, cols, tiles):
+            leaky(result_of[l][:, tiles, cols])
+            nc.sync.dma_start(out=out_by_l[l][:, tiles, cols], in_=result_of[l][:, tiles, cols])
+
         def finish_filter_half(l, half):
-            cols = slice(2 * P * half, 2 * P * (half + 1))
-            leaky(result_of[l][:, :, cols])
-            nc.sync.dma_start(out=out_by_l[l][:, :, cols], in_=result_of[l][:, :, cols])
+            finish_filter_cols(l, slice(2 * P * half, 2 * P * (half + 1)), slice(0, TILES))
 
         batch_norm_by_filter()
         for q, t in UNITS[:UNITS_AHEAD]:
             quantise_unit(q, t, turn_unit(q, t))
+        for n in range(UNITS_AHEAD, len(UNITS)):
+            if STEP_OF_UNIT[n] == 0:
+                sort_unit(*UNITS[n])
         rows = [(bn_scale[:].unsqueeze(2), scale_row)] + [(bn_shift[:, :, l : l + 1], shift_row[l]) for l in BATCH_MAJOR]
         squares_of = {0: repeat(rows[0][0]), 1: repeat(rows[1][0])}
 
@@ -301,6 +325,9 @@ def tile_residualblock5_pb_t_e_kernel(
             l, k = GROUPS[s]
             batch = l in BATCH_MAJOR
             turns = turns_after(s)
+            for n in range(UNITS_AHEAD, len(UNITS)):
+                if STEP_OF_UNIT[n] == s + 1:
+                    sort_unit(*UNITS[n])
             if s == HOLD:
                 waiting.extend(held)
             for item in waiting[: (1 if batch or turns else 2)]:
@@ -316,6 +343,9 @@ def tile_residualblock5_pb_t_e_kernel(
                 nc.vector.tensor_tensor(out=result_of[l][:, k, :], in0=acc[:], in1=scale_row[:], op=ALU.mult)
                 if k % 2 == 1:
                     (held if s < HOLD else waiting).extend([(add_x, l, k // 2), (finish_half, l, k // 2)])
+            elif s == len(GROUPS) - 1:
+                filter_products(l, k, interlude=lambda: turn_back(L - 1, TILES - 2), pieces=2)
+                finish_filter_cols(l, slice(P * (k - 1), P * k), slice(0, TILES))
             else:
                 filter_products(l, k)
             for l_turn, j in turns:
@@ -331,14 +361,22 @@ def tile_residualblock5_pb_t_e_kernel(
                 spread(squares_of[s + 1], rows[s + 1][1][:])
             if s + 2 < len(rows):
                 squares_of[s + 2] = repeat(rows[s + 2][0])
-            done = UNITS_AHEAD + UNITS_PER_STEP * s
-            units = [(q, t, turn_unit(q, t)) for q, t in UNITS[done : done + UNITS_PER_STEP]]
+            units = [UNITS[n] + (turn_unit(*UNITS[n]),) for n in range(UNITS_AHEAD, len(UNITS)) if STEP_OF_UNIT[n] == s]
             for q, t, grouped in units:
                 quantise_unit(q, t, grouped)
             if k == 0 and (l + 1 in BATCH_MAJOR or s == 0):
                 l_next = l if s == 0 else l + 1
                 (held if s < HOLD else waiting).extend([(shift_x, l_next, 0), (shift_x, l_next, 1)])
-        turn_back(L - 1, TILES - 1)
-        waiting.append((finish_filter_half, L - 1, 1))
         for item in waiting:
             item[0](item[1], item[2])
+        l, j = GROUPS[-1]
+        cols = slice(P * j, P * (j + 1))
+        for half in range(2):
+            tiles = slice(2 * half, 2 * half + 2)
+            bank = turn_pool.tile([P, 2, P], F32, tag="turn")
+            for t in range(2):
+                span = slice(P * (2 * half + t), P * (2 * half + t + 1))
+                nc.tensor.transpose(bank[:, t, :], normed_of[l, j][:, span], ident_f32[:])
+            nc.vector.tensor_tensor(out=result_of[l][:, tiles, cols], in0=bank[:], in1=x_sb[l][:, tiles, cols], op=ALU.add)
+        for half in range(2):
+            finish_filter_cols(l, cols, slice(2 * half, 2 * half + 2))

@@ -30,8 +30,9 @@ GROUPS = [(l, k) for l in range(L) for k in range(TILES)]
 UNITS = [(q, t) for t in range(TILES) for q in (0, 3)] + [(q, t) for q in (1, 2) for t in range(TILES)]
 UNITS_AHEAD = 4
 UNITS_PER_STEP = 2
+LATE_STEP = 6
 STEP_OF_UNIT = {
-    n: (n - UNITS_AHEAD) // UNITS_PER_STEP + (2 if n >= len(UNITS) - TILES else 0) for n in range(UNITS_AHEAD, len(UNITS))
+    n: LATE_STEP if n >= len(UNITS) - TILES else (n - UNITS_AHEAD) // UNITS_PER_STEP for n in range(UNITS_AHEAD, len(UNITS))
 }
 HOLD = 4
 
@@ -63,7 +64,7 @@ def tile_residualblock5_pb_t_e_kernel(
     with ExitStack() as ctx:
         ctx.enter_context(tc.manual_schedule())
         keep = ctx.enter_context(tc.tile_pool(name="keep", bufs=1))
-        stage = ctx.enter_context(tc.tile_pool(name="stage", bufs=3))
+        stage = ctx.enter_context(tc.tile_pool(name="stage", bufs=4))
         normed_pool = ctx.enter_context(tc.tile_pool(name="normed", bufs=6))
         sort_pool = ctx.enter_context(tc.tile_pool(name="sort", bufs=2 * UNITS_PER_STEP + 1))
         ahead = ctx.enter_context(tc.tile_pool(name="ahead", bufs=2))
@@ -84,10 +85,10 @@ def tile_residualblock5_pb_t_e_kernel(
         h_codes = [keep.tile([P, B], U32, name="h_codes%d" % m, align_bytes=64) for m in range(L)]
         h_scales = [keep.tile([P, B], U8, name="h_scales%d" % m, align_bytes=64) for m in range(L)]
 
+        nc.gpsimd.memset(params[:], 0.0)
         make_identity(nc, ident_f32[:])
         make_identity(nc, ident_bf16[:])
 
-        nc.vector.memset(params[:], 0.0)
         one = keep.tile([P, 1], F32, name="one")
         nc.vector.memset(one[:], 1.0)
         for l in range(L):
@@ -116,8 +117,8 @@ def tile_residualblock5_pb_t_e_kernel(
             nc.sync.dma_start(out=params[ROW_MEAN : ROW_MEAN + 1, :], in_=mean2.unsqueeze(0))
             nc.sync.dma_start(out=params[ROW_VAR : ROW_VAR + 1, :], in_=var2.unsqueeze(0))
 
-        load_params()
         load_h_ends(0)
+        load_params()
         load_h_ends(1)
         load_weights(0)
         nc.scalar.sqrt(out=one[:], in_=one[:])
@@ -178,11 +179,13 @@ def tile_residualblock5_pb_t_e_kernel(
 
         sorted_of = {}
 
-        def sort_unit(q, t):
+        def sort_unit(q, t, late):
             sorted_of[q, t] = sort_pool.tile([P, 2, 2, P], F32, name="sorted_words")
-            nc.vector.tensor_copy(
-                out=sorted_of[q, t][:], in_=h_raw[q][:, t, :].bitcast(F32).rearrange("p (e w u) -> p e u w", e=2, u=2)
-            )
+            words = h_raw[q][:, t, :].bitcast(F32).rearrange("p (e w u) -> p e u w", e=2, u=2)
+            if late:
+                nc.scalar.copy(out=sorted_of[q, t][:], in_=words)
+            else:
+                nc.vector.tensor_copy(out=sorted_of[q, t][:], in_=words)
 
         def turn_unit(q, t):
             words = h_raw[q][:, t, :].bitcast(F32)
@@ -309,12 +312,14 @@ def tile_residualblock5_pb_t_e_kernel(
         def finish_filter_half(l, half):
             finish_filter_cols(l, slice(2 * P * half, 2 * P * (half + 1)), slice(0, TILES))
 
+        for q, t in UNITS[: UNITS_AHEAD // 2]:
+            quantise_unit(q, t, turn_unit(q, t))
         batch_norm_by_filter()
-        for q, t in UNITS[:UNITS_AHEAD]:
+        for q, t in UNITS[UNITS_AHEAD // 2 : UNITS_AHEAD]:
             quantise_unit(q, t, turn_unit(q, t))
         for n in range(UNITS_AHEAD, len(UNITS)):
             if STEP_OF_UNIT[n] == 0:
-                sort_unit(*UNITS[n])
+                sort_unit(UNITS[n][0], UNITS[n][1], False)
         rows = [(bn_scale[:].unsqueeze(2), scale_row)] + [(bn_shift[:, :, l : l + 1], shift_row[l]) for l in BATCH_MAJOR]
         squares_of = {0: repeat(rows[0][0]), 1: repeat(rows[1][0])}
 
@@ -327,7 +332,7 @@ def tile_residualblock5_pb_t_e_kernel(
             turns = turns_after(s)
             for n in range(UNITS_AHEAD, len(UNITS)):
                 if STEP_OF_UNIT[n] == s + 1:
-                    sort_unit(*UNITS[n])
+                    sort_unit(UNITS[n][0], UNITS[n][1], s + 1 == LATE_STEP)
             if s == HOLD:
                 waiting.extend(held)
             for item in waiting[: (1 if batch or turns else 2)]:

@@ -30,7 +30,7 @@ GROUPS = [(l, k) for l in range(L) for k in range(TILES)]
 UNITS = [(q, t) for t in range(TILES) for q in (0, 3)] + [(q, t) for q in (1, 2) for t in range(TILES)]
 UNITS_AHEAD = 4
 UNITS_PER_STEP = 2
-LATE_STEP = 6
+LATE_STEP = 10
 STEP_OF_UNIT = {
     n: LATE_STEP if n >= len(UNITS) - TILES else (n - UNITS_AHEAD) // UNITS_PER_STEP for n in range(UNITS_AHEAD, len(UNITS))
 }
@@ -56,7 +56,7 @@ def tile_residualblock5_pb_t_e_kernel(
     nc = tc.nc
 
     h_pairs = h.rearrange("(t p) (q e) c -> p t q (e c)", p=P, e=2)
-    x_quads = x.rearrange("(t p) (g e) f -> g p t (e f)", p=P, e=4)
+    x_pairs = x.rearrange("(t p) (q e) f -> q p t (e f)", p=P, e=2)
     out_by_l = out.rearrange("(t p) l f -> l p t f", p=P)
     words_by_l = k2_words.bitcast(I32).rearrange("(i l) p w -> l p i w", l=L)
     scales_by_l = k2_scales.bitcast(I32).rearrange("(i l) (q r) n -> l r q i n", l=L, r=4)
@@ -101,9 +101,12 @@ def tile_residualblock5_pb_t_e_kernel(
             tiles = slice(2 * half, 2 * half + 2)
             nc.sync.dma_start(out=h_mid[:, q - 1, tiles], in_=h_pairs[:, tiles, q, :])
 
-        def load_x(g, half):
+        def load_x(q, half):
             tiles = slice(2 * half, 2 * half + 2)
-            nc.sync.dma_start(out=x_half[g][:, tiles].rearrange("p t e f -> p t (e f)"), in_=x_quads[g][:, tiles, :])
+            pair = slice(2 * (q % 2), 2 * (q % 2) + 2)
+            nc.sync.dma_start(
+                out=x_half[q // 2][:, tiles, pair, :].rearrange("p t e f -> p t (e f)"), in_=x_pairs[q][:, tiles, :]
+            )
 
         def load_weights(l):
             for r in range(4):
@@ -129,13 +132,17 @@ def tile_residualblock5_pb_t_e_kernel(
         load_weights(1)
         load_x(0, 0)
         load_x(0, 1)
+        load_weights(2)
         load_h_mid(2, 0)
         load_h_mid(2, 1)
-        load_weights(2)
-        load_weights(3)
         load_x(1, 0)
         load_x(1, 1)
-        for l in range(4, L):
+        load_weights(3)
+        load_weights(4)
+        for q in (2, 3):
+            load_x(q, 0)
+            load_x(q, 1)
+        for l in range(5, L):
             load_weights(l)
 
         def batch_norm_by_filter():

@@ -45,8 +45,8 @@ def turns_after(s):
     l, k = GROUPS[s]
     if l == L - 1 and k >= 2:
         return [(l, 0), (l, 1)] if k == 2 else []
-    if k == 0 and l >= 1 and l - 1 not in BATCH_MAJOR:
-        return [(l - 1, j) for j in range(TILES)]
+    if k < 2 and l >= 1 and l - 1 not in BATCH_MAJOR:
+        return [(l - 1, 2 * k), (l - 1, 2 * k + 1)]
     return []
 
 

@@ -45,8 +45,10 @@ def turns_after(s):
     l, k = GROUPS[s]
     if l == L - 1 and k >= 2:
         return [(l, 0), (l, 1)] if k == 2 else []
-    if k < 2 and l >= 1 and l - 1 not in BATCH_MAJOR:
-        return [(l - 1, 2 * k), (l - 1, 2 * k + 1)]
+    if k < 2 and l >= 1 and l not in BATCH_MAJOR:
+        before = l - 1 if l - 1 not in BATCH_MAJOR else l - 2
+        if before >= 1 and before not in BATCH_MAJOR:
+            return [(before, 2 * k), (before, 2 * k + 1)]
     return []
 
 
@@ -65,7 +67,7 @@ def tile_residualblock5_pb_t_e_kernel(
         ctx.enter_context(tc.manual_schedule())
         keep = ctx.enter_context(tc.tile_pool(name="keep", bufs=1))
         stage = ctx.enter_context(tc.tile_pool(name="stage", bufs=4))
-        normed_pool = ctx.enter_context(tc.tile_pool(name="normed", bufs=6))
+        normed_pool = ctx.enter_context(tc.tile_pool(name="normed", bufs=8))
         sort_pool = ctx.enter_context(tc.tile_pool(name="sort", bufs=2 * UNITS_PER_STEP + 1))
         ahead = ctx.enter_context(tc.tile_pool(name="ahead", bufs=2))
         out_pool = ctx.enter_context(tc.tile_pool(name="outs", bufs=4))

@@ -44,11 +44,11 @@ ROW_GAMMA, ROW_BETA, ROW_MEAN, ROW_VAR, PARAM_ROWS = L, L + 1, L + 2, L + 3, L +
 def turns_after(s):
     l, k = GROUPS[s]
     if l == L - 1 and k >= 2:
-        return [(l, 0), (l, 1)] if k == 2 else []
+        return [(l, 1)] if k == 2 else []
     if k < 2 and l >= 1 and l not in BATCH_MAJOR:
         before = l - 1 if l - 1 not in BATCH_MAJOR else l - 2
         if before >= 1 and before not in BATCH_MAJOR:
-            return [(before, 2 * k), (before, 2 * k + 1)]
+            return [(before, 2 * k), (before, 2 * k + 1)] + ([(l, 0)] if l == L - 1 and k == 1 else [])
     return []
 
 
@@ -318,8 +318,8 @@ def tile_residualblock5_pb_t_e_kernel(
             leaky(result_of[l][:, tiles, cols])
             nc.sync.dma_start(out=out_by_l[l][:, tiles, cols], in_=result_of[l][:, tiles, cols])
 
-        def finish_filter_half(l, half):
-            finish_filter_cols(l, slice(2 * P * half, 2 * P * (half + 1)), slice(0, TILES))
+        def finish_filter_tile(l, j):
+            finish_filter_cols(l, slice(P * j, P * (j + 1)), slice(0, TILES))
 
         for q, t in UNITS[: UNITS_AHEAD // 2]:
             quantise_unit(q, t, turn_unit(q, t))
@@ -369,8 +369,7 @@ def tile_residualblock5_pb_t_e_kernel(
                         waiting.append((finish_half, l_turn, j // 2))
                 else:
                     turn_back(l_turn, j)
-                    if j % 2 == 1:
-                        waiting.append((finish_filter_half, l_turn, j // 2))
+                    waiting.append((finish_filter_tile, l_turn, j))
             if 1 <= s < len(rows) - 1:
                 spread(squares_of[s + 1], rows[s + 1][1][:])
             if s + 2 < len(rows):

from contextlib import ExitStack

import concourse.mybir as mybir
from concourse.masks import make_identity

F32 = mybir.dt.float32
BF16 = mybir.dt.bfloat16
I32 = mybir.dt.int32
U32 = mybir.dt.uint32
U8 = mybir.dt.uint8
FP8X4 = mybir.dt.float8_e4m3fn_x4
FP4X4 = mybir.dt.float4_e2m1fn_x4
ALU = mybir.AluOpType
ACT = mybir.ActivationFunctionType

P = 128
B = 512
L = 8
C = 512
TAPS = 5
STEP = (0, 0, 1, -1, 2)
TAP_ORDER = (0, 1, 2, 4, 3)
BN_EPS = 1e-3
LEAKY_ALPHA = 0.3
TILES = 4

BATCH_MAJOR = (0, 3, 5)
GROUPS = [(l, k) for l in range(L) for k in range(TILES)]

UNITS = [(q, t) for t in range(TILES) for q in (0, 3)] + [(q, t) for q in (1, 2) for t in range(TILES)]
UNITS_AHEAD = 4
UNITS_PER_STEP = 2
LATE_STEP = 10
STEP_OF_UNIT = {
    n: LATE_STEP if n >= len(UNITS) - TILES else (n - UNITS_AHEAD) // UNITS_PER_STEP for n in range(UNITS_AHEAD, len(UNITS))
}
HOLD = 4

FLOPS = 2 * B * L * TAPS * C * C

ROW_GAMMA, ROW_BETA, ROW_MEAN, ROW_VAR, PARAM_ROWS = L, L + 1, L + 2, L + 3, L + 4


def turns_after(s):
    l, k = GROUPS[s]
    if l == L - 1 and k >= 2:
        return [(l, 1)] if k == 2 else []
    if k < 2 and l >= 1 and l not in BATCH_MAJOR:
        before = l - 1 if l - 1 not in BATCH_MAJOR else l - 2
        if before >= 1 and before not in BATCH_MAJOR:
            return [(before, 2 * k), (before, 2 * k + 1)] + ([(l, 0)] if l == L - 1 and k == 1 else [])
    return []


def tile_residualblock5_pb_t_e_kernel(
    tc, h, x, k2_words, k2_scales, b2, gamma2, beta2, mean2, var2, out
):
    nc = tc.nc

    h_pairs = h.rearrange("(t p) (q e) c -> p t q (e c)", p=P, e=2)
    x_pairs = x.rearrange("(t p) (q e) f -> q p t (e f)", p=P, e=2)
    out_by_l = out.rearrange("(t p) l f -> l p t f", p=P)
    words_by_l = k2_words.bitcast(I32).rearrange("(i l) p w -> l p i w", l=L)
    scales_by_l = k2_scales.bitcast(I32).rearrange("(i l) (q r) n -> l r q i n", l=L, r=4)

    with ExitStack() as ctx:
        ctx.enter_context(tc.manual_schedule())
        keep = ctx.enter_context(tc.tile_pool(name="keep", bufs=1))
        stage = ctx.enter_context(tc.tile_pool(name="stage", bufs=4))
        normed_pool = ctx.enter_context(tc.tile_pool(name="normed", bufs=8))
        sort_pool = ctx.enter_context(tc.tile_pool(name="sort", bufs=2 * UNITS_PER_STEP + 1))
        ahead = ctx.enter_context(tc.tile_pool(name="ahead", bufs=2))
        out_pool = ctx.enter_context(tc.tile_pool(name="outs", bufs=4))
        acc_pool = ctx.enter_context(tc.psum_pool(name="acc", bufs=4))
        turn_pool = ctx.enter_context(tc.psum_pool(name="turn", bufs=4))

        ident_f32 = keep.tile([P, P], F32, name="ident_f32")
        ident_bf16 = keep.tile([P, P], BF16, name="ident_bf16")
        params = keep.tile([P, C], BF16, name="params")
        h_ends = keep.tile([P, TILES, 2, 2 * C], BF16, name="h_ends")
        h_mid = keep.tile([P, 2, TILES, 2 * C], BF16, name="h_mid")
        h_raw = {0: h_ends[:, :, 0, :], 1: h_mid[:, 0], 2: h_mid[:, 1], 3: h_ends[:, :, 1, :]}
        x_half = [keep.tile([P, TILES, 4, C], BF16, name="x_half%d" % g) for g in range(2)]
        x_sb = [x_half[l // 4][:, :, l % 4, :] for l in range(L)]
        w_words = [keep.tile([P, TAPS, 2 * C], U8, name="w_words%d" % l, align_bytes=64) for l in range(L)]
        w_scales = [keep.tile([P, TAPS, C], U8, name="w_scales%d" % l, align_bytes=64) for l in range(L)]
        h_codes = [keep.tile([P, B], U32, name="h_codes%d" % m, align_bytes=64) for m in range(L)]
        h_scales = [keep.tile([P, B], U8, name="h_scales%d" % m, align_bytes=64) for m in range(L)]

        nc.gpsimd.memset(params[:], 0.0)
        make_identity(nc, ident_f32[:])
        make_identity(nc, ident_bf16[:])

        one = keep.tile([P, 1], F32, name="one")
        nc.vector.memset(one[:], 1.0)
        for l in range(L):
            nc.vector.memset(w_scales[l][:].bitcast(I32), 0)

        def load_h_ends(t):
            nc.sync.dma_start(out=h_ends[:, t], in_=h_pairs[:, t, 0:4:3, :])

        def load_h_mid(q, half):
            tiles = slice(2 * half, 2 * half + 2)
            nc.sync.dma_start(out=h_mid[:, q - 1, tiles], in_=h_pairs[:, tiles, q, :])

        def load_x(q, half):
            tiles = slice(2 * half, 2 * half + 2)
            pair = slice(2 * (q % 2), 2 * (q % 2) + 2)
            nc.sync.dma_start(
                out=x_half[q // 2][:, tiles, pair, :].rearrange("p t e f -> p t (e f)"), in_=x_pairs[q][:, tiles, :]
            )

        def load_weights(l):
            for r in range(4):
                nc.sync.dma_start(out=w_scales[l][r:P:32].bitcast(I32), in_=scales_by_l[l, r])
            nc.sync.dma_start(out=w_words[l][:].bitcast(I32), in_=words_by_l[l])

        def load_params():
            nc.sync.dma_start(out=params[0:L, :], in_=b2)
            nc.sync.dma_start(out=params[ROW_GAMMA : ROW_GAMMA + 1, :], in_=gamma2.unsqueeze(0))
            nc.sync.dma_start(out=params[ROW_BETA : ROW_BETA + 1, :], in_=beta2.unsqueeze(0))
            nc.sync.dma_start(out=params[ROW_MEAN : ROW_MEAN + 1, :], in_=mean2.unsqueeze(0))
            nc.sync.dma_start(out=params[ROW_VAR : ROW_VAR + 1, :], in_=var2.unsqueeze(0))

        load_h_ends(0)
        load_params()
        load_h_ends(1)
        load_weights(0)
        nc.scalar.sqrt(out=one[:], in_=one[:])
        load_h_ends(2)
        load_h_ends(3)
        load_h_mid(1, 0)
        load_h_mid(1, 1)
        load_weights(1)
        load_x(0, 0)
        load_x(0, 1)
        load_weights(2)
        load_h_mid(2, 0)
        load_h_mid(2, 1)
        load_x(1, 0)
        load_x(1, 1)
        load_weights(3)
        load_weights(4)
        for q in (2, 3):
            load_x(q, 0)
            load_x(q, 1)
        for l in range(5, L):
            load_weights(l)

        def batch_norm_by_filter():
            params_ps = turn_pool.tile([P, TILES, P], BF16, tag="turn")
            for j in range(TILES):
                nc.tensor.transpose(params_ps[:, j, :], params[:, P * j : P * (j + 1)], ident_bf16[:])
            nc.vector.tensor_copy(out=by_filter[:], in_=params_ps[:, :, 0:PARAM_ROWS])
            wide = [P, TILES, L]
            nc.vector.tensor_scalar_add(out=std[:], in0=by_filter[:, :, ROW_VAR], scalar1=BN_EPS)
            nc.scalar.sqrt(out=std[:], in_=std[:])
            nc.vector.reciprocal(out=bn_scale[:], in_=std[:])
            nc.vector.tensor_mul(out=bn_scale[:], in0=bn_scale[:], in1=by_filter[:, :, ROW_GAMMA])
            nc.vector.scalar_tensor_tensor(
                out=bn_shift[:],
                in0=by_filter[:, :, 0:L],
                scalar=2.0,
                in1=by_filter[:, :, ROW_MEAN : ROW_MEAN + 1].to_broadcast(wide),
                op0=ALU.mult,
                op1=ALU.subtract,
            )
            nc.vector.tensor_mul(out=bn_shift[:], in0=bn_shift[:], in1=bn_scale[:].unsqueeze(2).to_broadcast(wide))
            nc.vector.tensor_add(
                out=bn_shift[:], in0=bn_shift[:], in1=by_filter[:, :, ROW_BETA : ROW_BETA + 1].to_broadcast(wide)
            )

        by_filter = keep.tile([P, TILES, PARAM_ROWS], F32, name="by_filter")
        std = keep.tile([P, TILES], F32, name="std")
        bn_scale = keep.tile([P, TILES], F32, name="bn_scale")
        bn_shift = keep.tile([P, TILES, L], F32, name="bn_shift")

        def repeat(column):
            squares = ahead.tile([P, TILES, P], F32, name="squares")
            nc.scalar.copy(out=squares[:], in_=column.to_broadcast([P, TILES, P]))
            return squares

        def spread(squares, row):
            bank = turn_pool.tile([P, C], F32, tag="turn")
            for j in range(TILES):
                nc.tensor.transpose(bank[:, P * j : P * (j + 1)], squares[:, j, :], ident_f32[:])
            nc.scalar.copy(out=row, in_=bank[:])

        sorted_of = {}

        def sort_unit(q, t, late):
            sorted_of[q, t] = sort_pool.tile([P, 2, 2, P], F32, name="sorted_words")
            words = h_raw[q][:, t, :].bitcast(F32).rearrange("p (e w u) -> p e u w", e=2, u=2)
            if late:
                nc.scalar.copy(out=sorted_of[q, t][:], in_=words)
            else:
                nc.vector.tensor_copy(out=sorted_of[q, t][:], in_=words)

        def turn_unit(q, t):
            words = h_raw[q][:, t, :].bitcast(F32)
            bank = turn_pool.tile([P, 2, 2, P], F32, tag="turn")
            for e in range(2):
                for u in range(2):
                    if (q, t) in sorted_of:
                        nc.tensor.transpose(bank[:, e, u, :], sorted_of[q, t][:, e, u, :], ident_f32[:])
                    else:
                        nc.tensor.transpose(
                            bank[:, e, u, :], words[:, (C // 2) * e + u : (C // 2) * (e + 1) : 2], ident_f32[:]
                        )
            grouped = stage.tile([P, 2, 4 * P], BF16, name="grouped", align_bytes=64)
            nc.scalar.copy(
                out=grouped[:].bitcast(F32).rearrange("p e (b u) -> p e b u", u=2),
                in_=bank[:].rearrange("p e u b -> p e b u"),
            )
            return grouped

        def quantise_unit(q, t, grouped):
            for e in range(2):
                nc.vector.quantize_mx(
                    out=h_codes[2 * q + e][:, P * t : P * (t + 1)].bitcast(FP8X4),
                    scales=h_scales[2 * q + e][:, P * t : P * (t + 1)],
                    in_=grouped[:, e, :],
                )

        def leaky(values):
            nc.vector.scalar_tensor_tensor(
                out=values, in0=values, scalar=LEAKY_ALPHA, in1=values, op0=ALU.mult, op1=ALU.max
            )

        scale_row = keep.tile([P, C], F32, name="scale_row")
        shift_row = {}
        for l in BATCH_MAJOR:
            shift_row[l] = keep.tile([P, C], F32, name="shift_row%d" % l)
        x_shifted = keep.tile([P, TILES, C], F32, name="x_shifted")
        result_of = {}

        def shift_x(l, half):
            tiles = slice(2 * half, 2 * half + 2)
            nc.vector.tensor_tensor(
                out=x_shifted[:, tiles, :],
                in0=x_sb[l][:, tiles, :],
                in1=shift_row[l][:].unsqueeze(1).to_broadcast([P, 2, C]),
                op=ALU.add,
            )

        def batch_products(l, t):
            acc = acc_pool.tile([P, C], F32, tag="acc")
            for i in TAP_ORDER:
                m = (l - STEP[i]) % L
                nc.tensor.matmul_mx(
                    out=acc[:],
                    lhsT=h_codes[m][:, P * t : P * (t + 1)].bitcast(FP8X4),
                    lhsT_scale=h_scales[m][:, P * t : P * (t + 1)],
                    rhs=w_words[l][:, i, :].bitcast(FP4X4),
                    rhs_scale=w_scales[l][:, i, :],
                    start=(i == TAP_ORDER[0]),
                    stop=(i == TAP_ORDER[-1]),
                )
            return acc

        def add_x(l, half):
            tiles = slice(2 * half, 2 * half + 2)
            nc.vector.tensor_tensor(
                out=result_of[l][:, tiles, :], in0=result_of[l][:, tiles, :], in1=x_shifted[:, tiles, :], op=ALU.add
            )

        def finish_half(l, half):
            tiles = slice(2 * half, 2 * half + 2)
            leaky(result_of[l][:, tiles, :])
            nc.sync.dma_start(out=out_by_l[l][:, tiles, :], in_=result_of[l][:, tiles, :])

        normed_of = {}

        def filter_products(l, j, interlude=None, pieces=1):
            acc = acc_pool.tile([P, B], F32, tag="acc")
            for i in TAP_ORDER:
                if interlude is not None and i == TAP_ORDER[3]:
                    interlude()
                m = (l - STEP[i]) % L
                nc.tensor.matmul_mx(
                    out=acc[:],
                    lhsT=w_words[l][:, i, 2 * P * j : 2 * P * (j + 1)].bitcast(FP4X4),
                    lhsT_scale=w_scales[l][:, i, P * j : P * (j + 1)],
                    rhs=h_codes[m][:].bitcast(FP8X4),
                    rhs_scale=h_scales[m][:],
                    start=(i == TAP_ORDER[0]),
                    stop=(i == TAP_ORDER[-1]),
                )
            normed_of[l, j] = normed_pool.tile([P, B], F32, name="normed")
            for piece in range(pieces):
                span = slice(B // pieces * piece, B // pieces * (piece + 1))
                nc.scalar.activation(
                    out=normed_of[l, j][:, span],
                    in_=acc[:, span],
                    func=ACT.Identity,
                    bias=bn_shift[:, j, l : l + 1],
                    scale=bn_scale[:, j : j + 1],
                )

        def turn_back(l, j):
            if j == 0:
                result_of[l] = out_pool.tile([P, TILES, C], F32, name="result")
            bank = turn_pool.tile([P, TILES, P], F32, tag="turn")
            for t in range(TILES):
                nc.tensor.transpose(bank[:, t, :], normed_of[l, j][:, P * t : P * (t + 1)], ident_f32[:])
            cols = slice(P * j, P * (j + 1))
            nc.vector.tensor_tensor(out=result_of[l][:, :, cols], in0=bank[:], in1=x_sb[l][:, :, cols], op=ALU.add)

        def turn_back_tile(l, t):
            if t == 0:
                result_of[l] = out_pool.tile([P, TILES, C], F32, name="result")
            bank = turn_pool.tile([P, C], F32, tag="turn")
            for j in range(TILES):
                nc.tensor.transpose(bank[:, P * j : P * (j + 1)], normed_of[l, j][:, P * t : P * (t + 1)], ident_f32[:])
            nc.vector.tensor_tensor(out=result_of[l][:, t, :], in0=bank[:], in1=x_sb[l][:, t, :], op=ALU.add)

        def finish_filter_cols(l, cols, tiles):
            leaky(result_of[l][:, tiles, cols])
            nc.sync.dma_start(out=out_by_l[l][:, tiles, cols], in_=result_of[l][:, tiles, cols])

        def finish_filter_tile(l, j):
            finish_filter_cols(l, slice(P * j, P * (j + 1)), slice(0, TILES))

        for q, t in UNITS[: UNITS_AHEAD // 2]:
            quantise_unit(q, t, turn_unit(q, t))
        batch_norm_by_filter()
        for q, t in UNITS[UNITS_AHEAD // 2 : UNITS_AHEAD]:
            quantise_unit(q, t, turn_unit(q, t))
        for n in range(UNITS_AHEAD, len(UNITS)):
            if STEP_OF_UNIT[n] == 0:
                sort_unit(UNITS[n][0], UNITS[n][1], False)
        rows = [(bn_scale[:].unsqueeze(2), scale_row)] + [(bn_shift[:, :, l : l + 1], shift_row[l]) for l in BATCH_MAJOR]
        squares_of = {0: repeat(rows[0][0]), 1: repeat(rows[1][0])}

        waiting = []
        held = []

        for s in range(len(GROUPS)):
            l, k = GROUPS[s]
            batch = l in BATCH_MAJOR
            turns = turns_after(s)
            for n in range(UNITS_AHEAD, len(UNITS)):
                if STEP_OF_UNIT[n] == s + 1:
                    sort_unit(UNITS[n][0], UNITS[n][1], s + 1 == LATE_STEP)
            if s == HOLD:
                waiting.extend(held)
            for item in waiting[: (1 if batch or turns else 2)]:
                item[0](item[1], item[2])
                waiting.remove(item)
            if batch:
                if k == 0:
                    result_of[l] = out_pool.tile([P, TILES, C], F32, name="result")
                acc = batch_products(l, k)
                if s == 0:
                    spread(squares_of[0], rows[0][1][:])
                    spread(squares_of[1], rows[1][1][:])
                nc.vector.tensor_tensor(out=result_of[l][:, k, :], in0=acc[:], in1=scale_row[:], op=ALU.mult)
                if k % 2 == 1:
                    (held if s < HOLD else waiting).extend([(add_x, l, k // 2), (finish_half, l, k // 2)])
            elif s == len(GROUPS) - 1:
                filter_products(l, k, interlude=lambda: turn_back(L - 1, TILES - 2), pieces=2)
                finish_filter_cols(l, slice(P * (k - 1), P * k), slice(0, TILES))
            else:
                filter_products(l, k)
            for l_turn, j in turns:
                if l_turn < L - 1:
                    turn_back_tile(l_turn, j)
                    if j % 2 == 1:
                        waiting.append((finish_half, l_turn, j // 2))
                else:
                    turn_back(l_turn, j)
                    waiting.append((finish_filter_tile, l_turn, j))
            if 1 <= s < len(rows) - 1:
                spread(squares_of[s + 1], rows[s + 1][1][:])
            if s + 2 < len(rows):
                squares_of[s + 2] = repeat(rows[s + 2][0])
            units = [UNITS[n] + (turn_unit(*UNITS[n]),) for n in range(UNITS_AHEAD, len(UNITS)) if STEP_OF_UNIT[n] == s]
            for q, t, grouped in units:
                quantise_unit(q, t, grouped)
            if k == 0 and (l + 1 in BATCH_MAJOR or s == 0):
                l_next = l if s == 0 else l + 1
                (held if s < HOLD else waiting).extend([(shift_x, l_next, 0), (shift_x, l_next, 1)])
        for item in waiting:
            item[0](item[1], item[2])
        l, j = GROUPS[-1]
        cols = slice(P * j, P * (j + 1))
        for half in range(2):
            tiles = slice(2 * half, 2 * half + 2)
            bank = turn_pool.tile([P, 2, P], F32, tag="turn")
            for t in range(2):
                span = slice(P * (2 * half + t), P * (2 * half + t + 1))
                nc.tensor.transpose(bank[:, t, :], normed_of[l, j][:, span], ident_f32[:])
            nc.vector.tensor_tensor(out=result_of[l][:, tiles, cols], in0=bank[:], in1=x_sb[l][:, tiles, cols], op=ALU.add)
        for half in range(2):
            finish_filter_cols(l, cols, slice(2 * half, 2 * half + 2))
